import numpy as np
import ml_dtypes


def mxq(x, axis, fmt="e4m3"):
    dtype, down = {"e4m3": (ml_dtypes.float8_e4m3fn, 7), "e5m2": (ml_dtypes.float8_e5m2, 14)}[fmt]
    v = np.moveaxis(np.asarray(x, np.float32).astype(ml_dtypes.bfloat16).astype(np.float64), axis, -1)
    blocks = v.reshape(v.shape[:-1] + (-1, 32))
    amax = np.abs(blocks).max(-1, keepdims=True)
    byte = np.maximum(np.where(amax > 0, np.frexp(amax)[1] - 1 + 127, 0) - down, 1)
    scale = np.exp2(byte - 127.0)
    codes = (blocks / scale).astype(np.float32).astype(dtype).astype(np.float64)
    return np.moveaxis((codes * scale).reshape(v.shape), -1, axis)


WIDE = False


def mx_kscale(k):
    if not WIDE:
        return np.ones(k)
    levels = np.array([10, -10, 5, -5, 0])
    a = np.random.permutation(np.resize(levels, k // 512 * 4)).reshape(k // 512, 4)
    idx = np.arange(k)
    return np.exp2(a[idx // 512, idx % 128 // 32])


BF16 = ml_dtypes.bfloat16


def bf(x):
    return np.asarray(x, np.float32).astype(BF16)


def f64(x):
    return np.asarray(x).astype(np.float64)


S, B, H, D, LOCAL, BQ, BK, G = 2048, 1, 8, 128, 1024, 16, 128, 512
NEG = -10000.0
QC = 4.0


def span(g):
    hi = (g + 1) * BK
    lo = max(hi - LOCAL, 0)
    return lo, lo + -(-(hi - lo) // G) * G


def masked(sid, tid):
    qr = (sid // BQ * BQ)[:, None]
    kr = (tid // BK * BK)[None, :]
    return (qr < kr) | (qr >= kr + LOCAL) | (sid[:, None] < tid[None, :])


def setup_inputs():
    shape = (S, B, H, D)
    t = f64(mx_kscale(S))
    t.reshape(-1, BK)[:, :BK // 4] = t.max()
    q = np.random.standard_normal(shape)
    k = np.random.standard_normal(shape)
    v = np.random.standard_normal(shape) * 2.0
    q[..., 0] = QC
    k[..., 0] += (np.log(t) * np.sqrt(D) / QC)[:, None, None]
    v *= (t.max() / t)[:, None, None, None]
    return {"q_rot": bf(q), "k_rot": bf(k), "v": bf(v)}


def reference(q_rot, k_rot, v):
    q = f64(q_rot).transpose(1, 2, 0, 3)
    kt = f64(k_rot).transpose(1, 2, 3, 0)
    vq = mxq(f64(v).transpose(1, 2, 0, 3), 2, "e4m3")
    norm = 1.0 / np.sqrt(D)
    outs = []
    for g in range(S // BK):
        r0, r1 = g * BK, (g + 1) * BK
        lo, hi = span(g)
        s = q[:, :, r0:r1] @ kt[:, :, :, lo:hi] * norm
        s = np.where(masked(np.arange(r0, r1), np.arange(lo, hi))[None, None], NEG, s)
        e = np.exp(s - s.max(-1, keepdims=True))
        outs.append((mxq(e, 3, "e4m3") @ vq[:, :, lo:hi]) / e.sum(-1, keepdims=True))
    ctx = np.concatenate(outs, axis=2)
    return ctx.transpose(2, 0, 1, 3).reshape(S, B, H * D)

@@ -1,0 +1,325 @@
+from contextlib import ExitStack
+
+import concourse.mybir as mybir
+from concourse.masks import make_identity
+
+BF16 = mybir.dt.bfloat16
+F32 = mybir.dt.float32
+I32 = mybir.dt.int32
+U32 = mybir.dt.uint32
+U8 = mybir.dt.uint8
+FP8X4 = mybir.dt.float8_e4m3fn_x4
+ALU = mybir.AluOpType
+ACT = mybir.ActivationFunctionType
+AXIS_X = mybir.AxisListType.X
+
+S = 2048
+H = 8
+D = 128
+P = 128
+PACK = 4
+GROUPS = S // P
+RING = 8
+HALF = 4
+K_PASS = HALF * P
+BATCH = 4
+NORM = 1.0 / (D**0.5)
+MASKED = -1.0e10
+E_BUFFERS = 3
+WINDOWS = S // K_PASS
+
+LAG_EXP = 1
+LAG_TURN = 2
+LAG_QUANT = 3
+LAG_PV = 4
+LAG_STORE = 5
+
+FLOPS = 2 * 2 * H * P * D * (4 * K_PASS + 12 * 2 * K_PASS)
+
+
+def ring_block(g, slot):
+    return g - (g - slot) % RING
+
+
+def passes_of(g):
+    return 1 if g < HALF else 2
+
+
+def tile_sparseselfattention_pa_kernel(tc, q_rot, k_rot, v, out):
+    nc = tc.nc
+    q2d = q_rot.rearrange("s b h d -> s (b h d)")
+    k2d = k_rot.rearrange("s b h d -> s (b h d)")
+    v2d = v.rearrange("s b h d -> s (b h d)")
+    out2d = out.rearrange("s b c -> s (b c)")
+    units = [(g, h) for g in range(GROUPS) for h in range(H)]
+
+    with ExitStack() as ctx:
+        const = ctx.enter_context(tc.tile_pool(name="const", bufs=1))
+        turned = ctx.enter_context(tc.tile_pool(name="turned", bufs=2))
+        work = ctx.enter_context(tc.tile_pool(name="work", bufs=3))
+        small = ctx.enter_context(tc.tile_pool(name="small", bufs=3))
+        score_banks = ctx.enter_context(tc.psum_pool(name="score_banks", bufs=4))
+        turn_banks = ctx.enter_context(tc.psum_pool(name="turn_banks", bufs=2))
+        ctx_banks = ctx.enter_context(tc.psum_pool(name="ctx_banks", bufs=2))
+        ctx.enter_context(tc.manual_schedule())
+
+        q_rows = {}
+        k_rows = {}
+        v_rows = {}
+        for g in range(GROUPS):
+            for name, src, rows in (("q", q2d, q_rows), ("k", k2d, k_rows)):
+                rows[g] = const.tile([P, H * D], BF16, name="%s_rows_%d" % (name, g))
+                nc.sync.dma_start(out=rows[g][:], in_=src[g * P : (g + 1) * P, :])
+            if g % 2 == 0 and g // 2 < WINDOWS:
+                w = g // 2
+                v_rows[w] = const.tile([P, PACK, H * D], BF16, name="v_rows_%d" % w)
+                nc.sync.dma_start(
+                    out=v_rows[w][:],
+                    in_=v2d[w * K_PASS : (w + 1) * K_PASS, :].rearrange("(p j) c -> p j c", j=PACK),
+                )
+
+        ident_bf = const.tile([P, P], BF16)
+        make_identity(nc, ident_bf[:])
+        ident_f32 = const.tile([P, P], F32)
+        make_identity(nc, ident_f32[:])
+        causal_f32 = const.tile([P, P], F32)
+        nc.gpsimd.memset(causal_f32[:], 0.0)
+        nc.gpsimd.affine_select(
+            out=causal_f32[:],
+            in_=causal_f32[:],
+            compare_op=ALU.is_ge,
+            fill=MASKED,
+            base=0,
+            pattern=[[-1, P]],
+            channel_multiplier=1,
+        )
+        causal_bf = const.tile([P, P], BF16)
+        nc.vector.tensor_copy(out=causal_bf[:], in_=causal_f32[:])
+
+        e_tiles = []
+        for i in range(E_BUFFERS):
+            halves = []
+            for c in range(RING // HALF):
+                e_half = const.tile([P, K_PASS], BF16, name="e_%d_%d" % (i, c))
+                nc.vector.memset(e_half[:], 0.0)
+                halves.append(e_half)
+            e_tiles.append(halves)
+
+        v_codes = [const.tile([P, H * D], U32, align_bytes=64, name="v_codes_%d" % w) for w in range(WINDOWS)]
+        v_scales = [const.tile([P, H * D], U8, align_bytes=64, name="v_scales_%d" % w) for w in range(WINDOWS)]
+
+        q_turned = {}
+        k_turned = {}
+        banks = {}
+        widths = {}
+        maxima = {}
+        bias = {}
+        row_sums = {}
+        e_turned = {}
+        e_grouped = {}
+        e_codes = {}
+        e_scales = {}
+        ctx_bank = {}
+        v_grouped = {}
+        totals = {}
+        inverse = {}
+
+        def turn_q(g):
+            bank = turn_banks.tile([P, H, P], BF16, tag="turn", name="q_bank")
+            for h in range(H):
+                nc.tensor.transpose(bank[:, h, :], q_rows[g][:, h * D : (h + 1) * D], ident_bf[:])
+            q_turned[g] = turned.tile([P, H, P], BF16, name="qT")
+            nc.vector.tensor_copy(out=q_turned[g][:], in_=bank[:])
+
+        def turn_k(b):
+            bank = turn_banks.tile([P, H, P], BF16, tag="turn", name="k_bank")
+            for h in range(H):
+                nc.tensor.transpose(bank[:, h, :], k_rows[b][:, h * D : (h + 1) * D], ident_bf[:])
+            k_turned[b] = turned.tile([P, H, P], BF16, name="kT", bufs=RING + 2)
+            nc.scalar.copy(out=k_turned[b][:], in_=bank[:])
+
+        def scores(j):
+            g, h = units[j]
+            banks[j] = []
+            widths[j] = []
+            for c in range(passes_of(g)):
+                bank = score_banks.tile([P, K_PASS], F32, name="score_bank")
+                live = [s for s in range(c * HALF, (c + 1) * HALF) if ring_block(g, s) >= 0]
+                for s in live:
+                    b = ring_block(g, s)
+                    cols = slice((s % HALF) * P, (s % HALF + 1) * P)
+                    nc.tensor.matmul(
+                        bank[:, cols], lhsT=q_turned[g][:, h, :], rhs=k_turned[b][:, h, :],
+                        start=True, stop=(b != g),
+                    )
+                    if b == g:
+                        nc.tensor.matmul(
+                            bank[:, cols], lhsT=ident_bf[:], rhs=causal_bf[:], start=False, stop=True
+                        )
+                banks[j].append(bank)
+                widths[j].append(len(live) * P)
+
+        def row_maximum(j, c):
+            g, h = units[j]
+            if c == 0:
+                maxima[j] = small.tile([P, passes_of(g)], F32, name="maxima")
+            if c < passes_of(g):
+                nc.vector.tensor_reduce(
+                    out=maxima[j][:, c : c + 1], in_=banks[j][c][:, : widths[j][c]], axis=AXIS_X, op=ALU.max
+                )
+
+        def exp_bias(j):
+            g, h = units[j]
+            bias[j] = small.tile([P, 1], F32, name="bias")
+            if passes_of(g) == 2:
+                nc.vector.tensor_scalar(
+                    out=bias[j][:], in0=maxima[j][:, 0:1], scalar1=maxima[j][:, 1:2], scalar2=-NORM,
+                    op0=ALU.max, op1=ALU.mult,
+                )
+            else:
+                nc.vector.tensor_scalar(
+                    out=bias[j][:], in0=maxima[j][:, 0:1], scalar1=-NORM, scalar2=None, op0=ALU.mult
+                )
+
+        def exponentials(j):
+            g, h = units[j]
+            batch = j // BATCH
+            if j % BATCH == 0:
+                row_sums[batch] = small.tile([P, BATCH, passes_of(g)], F32, name="row_sums")
+            for c in range(passes_of(g)):
+                nc.scalar.activation(
+                    out=e_tiles[j % E_BUFFERS][c][:, : widths[j][c]], in_=banks[j][c][:, : widths[j][c]],
+                    func=ACT.Exp, bias=bias[j][:, 0:1], scale=NORM,
+                    accum_out=row_sums[batch][:, j % BATCH, c : c + 1],
+                )
+
+        def turn_e(j):
+            g, h = units[j]
+            e_turned[j] = turn_banks.tile([P, passes_of(g), 2, P], F32, tag="turn", name="e_turned")
+            for c in range(passes_of(g)):
+                words = e_tiles[j % E_BUFFERS][c][:].bitcast(F32).rearrange("q (p u) -> q u p", u=2)
+                for u in range(2):
+                    nc.tensor.transpose(e_turned[j][:, c, u, :], words[:, u, :], ident_f32[:])
+
+        def regroup_e(j):
+            g, h = units[j]
+            e_grouped[j] = work.tile([P, passes_of(g) * P * PACK], BF16, align_bytes=64, name="e_grouped")
+            nc.scalar.copy(
+                out=e_grouped[j][:].bitcast(F32).rearrange("p (c q u) -> p c q u", c=passes_of(g), u=2),
+                in_=e_turned[j][:].rearrange("p c u q -> p c q u"),
+            )
+
+        def quantise_e(j):
+            g, h = units[j]
+            e_codes[j] = work.tile([P, passes_of(g) * P], U32, align_bytes=64, name="e_codes")
+            e_scales[j] = work.tile([P, passes_of(g) * P], U8, align_bytes=64, name="e_scales")
+            nc.vector.quantize_mx(
+                out=e_codes[j][:].bitcast(FP8X4), scales=e_scales[j][:], in_=e_grouped[j][:]
+            )
+
+        def e_times_v(j):
+            g, h = units[j]
+            batch = j // BATCH
+            if j % BATCH == 0:
+                ctx_bank[batch] = ctx_banks.tile([P, BATCH * D], F32, name="ctx_bank")
+            for c in range(passes_of(g)):
+                nc.tensor.matmul_mx(
+                    out=ctx_bank[batch][:, (j % BATCH) * D : (j % BATCH + 1) * D],
+                    lhsT=e_codes[j][:, c * P : (c + 1) * P].bitcast(FP8X4),
+                    lhsT_scale=e_scales[j][:, c * P : (c + 1) * P],
+                    rhs=v_codes[c][:, h * D : (h + 1) * D].bitcast(FP8X4),
+                    rhs_scale=v_scales[c][:, h * D : (h + 1) * D],
+                    start=(c == 0),
+                    stop=(c == passes_of(g) - 1),
+                )
+
+        def regroup_v(w, h):
+            v_grouped[w, h] = work.tile([P, D, PACK], BF16, align_bytes=64, name="v_grouped")
+            nc.vector.tensor_copy(
+                out=v_grouped[w, h][:].rearrange("p (c i) j -> p c j i", i=4),
+                in_=v_rows[w][:, :, h * D : (h + 1) * D].rearrange("p j (c i) -> p c j i", i=4),
+            )
+
+        def quantise_v(w, h):
+            nc.vector.quantize_mx(
+                out=v_codes[w][:, h * D : (h + 1) * D].bitcast(FP8X4),
+                scales=v_scales[w][:, h * D : (h + 1) * D],
+                in_=v_grouped[w, h][:].rearrange("p c j -> p (c j)"),
+            )
+
+        def enter_ring(b):
+            rows = slice((b % HALF) * 32, (b % HALF) * 32 + 32)
+            half = (b // HALF) % 2
+            nc.vector.tensor_copy(
+                out=v_codes[half][rows, :].bitcast(I32), in_=v_codes[b // HALF][rows, :].bitcast(I32)
+            )
+            nc.vector.tensor_copy(
+                out=v_scales[half][rows, :].bitcast(I32), in_=v_scales[b // HALF][rows, :].bitcast(I32)
+            )
+
+        def sum_rows(batch):
+            totals[batch] = small.tile([P, BATCH], F32, name="totals")
+            nc.vector.tensor_reduce(out=totals[batch][:], in_=row_sums[batch][:], axis=AXIS_X, op=ALU.add)
+
+        def invert_sums(batch):
+            inverse[batch] = small.tile([P, BATCH], F32, name="inverse")
+            nc.vector.reciprocal(out=inverse[batch][:], in_=totals[batch][:])
+
+        def divide_and_store(batch):
+            g, first_head = units[batch * BATCH]
+            result = work.tile([P, BATCH, D], F32, name="result")
+            nc.vector.tensor_tensor(
+                out=result[:],
+                in0=ctx_bank[batch][:].rearrange("q (h d) -> q h d", h=BATCH),
+                in1=inverse[batch][:].unsqueeze(2).to_broadcast([P, BATCH, D]),
+                op=ALU.mult,
+            )
+            nc.sync.dma_start(
+                out=out2d[g * P : (g + 1) * P, first_head * D : (first_head + BATCH) * D],
+                in_=result[:].rearrange("q h d -> q (h d)"),
+            )
+
+        def is_unit(j):
+            return 0 <= j < len(units)
+
+        turn_q(0)
+        turn_k(0)
+        for j in range(len(units) + LAG_STORE + 1):
+            closing = (j - LAG_STORE) // BATCH if is_unit(j - LAG_STORE) and (j - LAG_STORE) % BATCH == BATCH - 1 else None
+            window = None
+            if is_unit(j) and (units[j][0] == 0 or (units[j][0] + 2) % HALF == 0) and (units[j][0] + 2) // HALF < WINDOWS:
+                window = (units[j][0] + 2) // HALF
+
+            if is_unit(j):
+                scores(j)
+                row_maximum(j, 0)
+            if closing is not None:
+                sum_rows(closing)
+            if window is not None:
+                regroup_v(window, units[j][1])
+            if is_unit(j):
+                row_maximum(j, 1)
+            if closing is not None:
+                invert_sums(closing)
+            if is_unit(j - LAG_QUANT):
+                quantise_e(j - LAG_QUANT)
+            if window is not None:
+                quantise_v(window, units[j][1])
+            if is_unit(j):
+                exp_bias(j)
+            if is_unit(j - LAG_EXP):
+                exponentials(j - LAG_EXP)
+            if is_unit(j - LAG_PV):
+                e_times_v(j - LAG_PV)
+            if is_unit(j - LAG_TURN):
+                turn_e(j - LAG_TURN)
+                regroup_e(j - LAG_TURN)
+            if is_unit(j + 1 - LAG_PV) and units[j + 1 - LAG_PV][0] >= RING and units[j + 1 - LAG_PV][1] == 0:
+                enter_ring(units[j + 1 - LAG_PV][0])
+            if closing is not None:
+                divide_and_store(closing)
+            if is_unit(j) and units[j][0] + 1 < GROUPS:
+                if units[j][1] == 1:
+                    turn_q(units[j][0] + 1)
+                if units[j][1] == 3:
+                    turn_k(units[j][0] + 1)

@@ -11,7 +11,6 @@ U8 = mybir.dt.uint8
 FP8X4 = mybir.dt.float8_e4m3fn_x4
 ALU = mybir.AluOpType
 ACT = mybir.ActivationFunctionType
-AXIS_X = mybir.AxisListType.X
 
 S = 2048
 H = 8
@@ -22,11 +21,12 @@ GROUPS = S // P
 RING = 8
 HALF = 4
 K_PASS = HALF * P
+LANES = 2
 BATCH = 4
+WINDOWS = S // K_PASS
 NORM = 1.0 / (D**0.5)
 MASKED = -1.0e10
 E_BUFFERS = 3
-WINDOWS = S // K_PASS
 
 LAG_EXP = 1
 LAG_TURN = 2
@@ -41,8 +41,8 @@ def ring_block(g, slot):
     return g - (g - slot) % RING
 
 
-def passes_of(g):
-    return 1 if g < HALF else 2
+def live_slots(g, half):
+    return [s for s in range(half * HALF, (half + 1) * HALF) if ring_block(g, s) >= 0]
 
 
 def tile_sparseselfattention_pa_kernel(tc, q_rot, k_rot, v, out):
@@ -51,13 +51,44 @@ def tile_sparseselfattention_pa_kernel(tc, q_rot, k_rot, v, out):
     k2d = k_rot.rearrange("s b h d -> s (b h d)")
     v2d = v.rearrange("s b h d -> s (b h d)")
     out2d = out.rearrange("s b c -> s (b c)")
-    units = [(g, h) for g in range(GROUPS) for h in range(H)]
+
+    units = []
+    lanes = []
+    for g in range(GROUPS):
+        if g < HALF:
+            for h in range(0, H, LANES):
+                units.append((g, (h, h + 1)))
+                lanes.append(((h, 0), (h + 1, 0)))
+        else:
+            for h in range(H):
+                units.append((g, (h,)))
+                lanes.append(((h, 0), (h, 1)))
+
+    def is_unit(j):
+        return 0 <= j < len(units)
+
+    def batch_of(j):
+        return (units[j][0], units[j][1][0] // BATCH)
+
+    def opens_batch(j):
+        return units[j][1][0] % BATCH == 0
+
+    def ends_batch(j):
+        return is_unit(j) and units[j][1][-1] % BATCH == BATCH - 1
+
+    def window_of(j):
+        if not is_unit(j):
+            return None
+        g = units[j][0]
+        if (g == 0 or (g + 2) % HALF == 0) and (g + 2) // HALF < WINDOWS:
+            return (g + 2) // HALF
+        return None
 
     with ExitStack() as ctx:
         const = ctx.enter_context(tc.tile_pool(name="const", bufs=1))
         turned = ctx.enter_context(tc.tile_pool(name="turned", bufs=2))
         work = ctx.enter_context(tc.tile_pool(name="work", bufs=3))
-        small = ctx.enter_context(tc.tile_pool(name="small", bufs=3))
+        small = ctx.enter_context(tc.tile_pool(name="small", bufs=4))
         score_banks = ctx.enter_context(tc.psum_pool(name="score_banks", bufs=4))
         turn_banks = ctx.enter_context(tc.psum_pool(name="turn_banks", bufs=2))
         ctx_banks = ctx.enter_context(tc.psum_pool(name="ctx_banks", bufs=2))
@@ -96,14 +127,11 @@ def tile_sparseselfattention_pa_kernel(tc, q_rot, k_rot, v, out):
         causal_bf = const.tile([P, P], BF16)
         nc.vector.tensor_copy(out=causal_bf[:], in_=causal_f32[:])
 
-        e_tiles = []
-        for i in range(E_BUFFERS):
-            halves = []
-            for c in range(RING // HALF):
-                e_half = const.tile([P, K_PASS], BF16, name="e_%d_%d" % (i, c))
-                nc.vector.memset(e_half[:], 0.0)
-                halves.append(e_half)
-            e_tiles.append(halves)
+        e_tiles = {}
+        for heads in (1, 2):
+            for i in range(E_BUFFERS):
+                e_tiles[heads, i] = const.tile([P, LANES * K_PASS], BF16, name="e_%d_%d" % (heads, i))
+                nc.vector.memset(e_tiles[heads, i][:], 0.0)
 
         v_codes = [const.tile([P, H * D], U32, align_bytes=64, name="v_codes_%d" % w) for w in range(WINDOWS)]
         v_scales = [const.tile([P, H * D], U8, align_bytes=64, name="v_scales_%d" % w) for w in range(WINDOWS)]
@@ -112,7 +140,8 @@ def tile_sparseselfattention_pa_kernel(tc, q_rot, k_rot, v, out):
         k_turned = {}
         banks = {}
         widths = {}
-        maxima = {}
+        negated = {}
+        minima = {}
         bias = {}
         row_sums = {}
         e_turned = {}
@@ -121,8 +150,10 @@ def tile_sparseselfattention_pa_kernel(tc, q_rot, k_rot, v, out):
         e_scales = {}
         ctx_bank = {}
         v_grouped = {}
-        totals = {}
         inverse = {}
+
+        def e_tile(j):
+            return e_tiles[len(units[j][1]), j % E_BUFFERS]
 
         def turn_q(g):
             bank = turn_banks.tile([P, H, P], BF16, tag="turn", name="q_bank")
@@ -139,13 +170,12 @@ def tile_sparseselfattention_pa_kernel(tc, q_rot, k_rot, v, out):
             nc.scalar.copy(out=k_turned[b][:], in_=bank[:])
 
         def scores(j):
-            g, h = units[j]
+            g = units[j][0]
             banks[j] = []
             widths[j] = []
-            for c in range(passes_of(g)):
+            for h, half in lanes[j]:
                 bank = score_banks.tile([P, K_PASS], F32, name="score_bank")
-                live = [s for s in range(c * HALF, (c + 1) * HALF) if ring_block(g, s) >= 0]
-                for s in live:
+                for s in live_slots(g, half):
                     b = ring_block(g, s)
                     cols = slice((s % HALF) * P, (s % HALF + 1) * P)
                     nc.tensor.matmul(
@@ -157,94 +187,98 @@ def tile_sparseselfattention_pa_kernel(tc, q_rot, k_rot, v, out):
                             bank[:, cols], lhsT=ident_bf[:], rhs=causal_bf[:], start=False, stop=True
                         )
                 banks[j].append(bank)
-                widths[j].append(len(live) * P)
+                widths[j].append(len(live_slots(g, half)) * P)
 
-        def row_maximum(j, c):
-            g, h = units[j]
-            if c == 0:
-                maxima[j] = small.tile([P, passes_of(g)], F32, name="maxima")
-            if c < passes_of(g):
-                nc.vector.tensor_reduce(
-                    out=maxima[j][:, c : c + 1], in_=banks[j][c][:, : widths[j][c]], axis=AXIS_X, op=ALU.max
+        def negate_and_minimum(j):
+            negated[j] = work.tile([P, LANES * K_PASS], F32, name="negated", bufs=4)
+            minima[j] = small.tile([P, LANES], F32, name="minima")
+            for lane in range(LANES):
+                nc.vector.tensor_scalar(
+                    out=negated[j][:, lane * K_PASS : lane * K_PASS + widths[j][lane]],
+                    in0=banks[j][lane][:, : widths[j][lane]],
+                    scalar1=-NORM, scalar2=None, op0=ALU.mult, op1=ALU.min,
+                    accum_out=minima[j][:, lane : lane + 1],
                 )
 
         def exp_bias(j):
-            g, h = units[j]
-            bias[j] = small.tile([P, 1], F32, name="bias")
-            if passes_of(g) == 2:
-                nc.vector.tensor_scalar(
-                    out=bias[j][:], in0=maxima[j][:, 0:1], scalar1=maxima[j][:, 1:2], scalar2=-NORM,
-                    op0=ALU.max, op1=ALU.mult,
-                )
-            else:
-                nc.vector.tensor_scalar(
-                    out=bias[j][:], in0=maxima[j][:, 0:1], scalar1=-NORM, scalar2=None, op0=ALU.mult
+            if len(units[j][1]) == 1:
+                bias[j] = small.tile([P, 1], F32, name="bias")
+                nc.vector.tensor_tensor(
+                    out=bias[j][:], in0=minima[j][:, 0:1], in1=minima[j][:, 1:2], op=ALU.min
                 )
 
         def exponentials(j):
-            g, h = units[j]
-            batch = j // BATCH
-            if j % BATCH == 0:
-                row_sums[batch] = small.tile([P, BATCH, passes_of(g)], F32, name="row_sums")
-            for c in range(passes_of(g)):
+            heads = units[j][1]
+            if opens_batch(j):
+                row_sums[batch_of(j)] = small.tile([P, BATCH], F32, name="row_sums")
+            sums = row_sums[batch_of(j)]
+            if len(heads) == 1:
+                width = K_PASS + widths[j][1]
                 nc.scalar.activation(
-                    out=e_tiles[j % E_BUFFERS][c][:, : widths[j][c]], in_=banks[j][c][:, : widths[j][c]],
-                    func=ACT.Exp, bias=bias[j][:, 0:1], scale=NORM,
-                    accum_out=row_sums[batch][:, j % BATCH, c : c + 1],
+                    out=e_tile(j)[:, :width], in_=negated[j][:, :width], func=ACT.Exp,
+                    bias=bias[j][:, 0:1], scale=-1.0,
+                    accum_out=sums[:, heads[0] % BATCH : heads[0] % BATCH + 1],
                 )
+            else:
+                for lane in range(LANES):
+                    cols = slice(lane * K_PASS, lane * K_PASS + widths[j][lane])
+                    nc.scalar.activation(
+                        out=e_tile(j)[:, cols], in_=negated[j][:, cols], func=ACT.Exp,
+                        bias=minima[j][:, lane : lane + 1], scale=-1.0,
+                        accum_out=sums[:, heads[lane] % BATCH : heads[lane] % BATCH + 1],
+                    )
 
         def turn_e(j):
-            g, h = units[j]
-            e_turned[j] = turn_banks.tile([P, passes_of(g), 2, P], F32, tag="turn", name="e_turned")
-            for c in range(passes_of(g)):
-                words = e_tiles[j % E_BUFFERS][c][:].bitcast(F32).rearrange("q (p u) -> q u p", u=2)
+            e_turned[j] = turn_banks.tile([P, LANES, 2, P], F32, tag="turn", name="e_turned")
+            words = e_tile(j)[:].bitcast(F32).rearrange("q (l p u) -> q l u p", l=LANES, u=2)
+            for lane in range(LANES):
                 for u in range(2):
-                    nc.tensor.transpose(e_turned[j][:, c, u, :], words[:, u, :], ident_f32[:])
+                    nc.tensor.transpose(e_turned[j][:, lane, u, :], words[:, lane, u, :], ident_f32[:])
 
         def regroup_e(j):
-            g, h = units[j]
-            e_grouped[j] = work.tile([P, passes_of(g) * P * PACK], BF16, align_bytes=64, name="e_grouped")
+            e_grouped[j] = work.tile([P, LANES * P * PACK], BF16, align_bytes=64, name="e_grouped")
             nc.scalar.copy(
-                out=e_grouped[j][:].bitcast(F32).rearrange("p (c q u) -> p c q u", c=passes_of(g), u=2),
-                in_=e_turned[j][:].rearrange("p c u q -> p c q u"),
+                out=e_grouped[j][:].bitcast(F32).rearrange("p (l q u) -> p l q u", l=LANES, u=2),
+                in_=e_turned[j][:].rearrange("p l u q -> p l q u"),
             )
 
         def quantise_e(j):
-            g, h = units[j]
-            e_codes[j] = work.tile([P, passes_of(g) * P], U32, align_bytes=64, name="e_codes")
-            e_scales[j] = work.tile([P, passes_of(g) * P], U8, align_bytes=64, name="e_scales")
+            e_codes[j] = work.tile([P, LANES * P], U32, align_bytes=64, name="e_codes")
+            e_scales[j] = work.tile([P, LANES * P], U8, align_bytes=64, name="e_scales")
             nc.vector.quantize_mx(
                 out=e_codes[j][:].bitcast(FP8X4), scales=e_scales[j][:], in_=e_grouped[j][:]
             )
 
         def e_times_v(j):
-            g, h = units[j]
-            batch = j // BATCH
-            if j % BATCH == 0:
-                ctx_bank[batch] = ctx_banks.tile([P, BATCH * D], F32, name="ctx_bank")
-            for c in range(passes_of(g)):
+            one_head = len(units[j][1]) == 1
+            if opens_batch(j):
+                ctx_bank[batch_of(j)] = ctx_banks.tile([P, BATCH * D], F32, name="ctx_bank")
+            for lane in range(LANES):
+                h, half = lanes[j][lane]
                 nc.tensor.matmul_mx(
-                    out=ctx_bank[batch][:, (j % BATCH) * D : (j % BATCH + 1) * D],
-                    lhsT=e_codes[j][:, c * P : (c + 1) * P].bitcast(FP8X4),
-                    lhsT_scale=e_scales[j][:, c * P : (c + 1) * P],
-                    rhs=v_codes[c][:, h * D : (h + 1) * D].bitcast(FP8X4),
-                    rhs_scale=v_scales[c][:, h * D : (h + 1) * D],
-                    start=(c == 0),
-                    stop=(c == passes_of(g) - 1),
+                    out=ctx_bank[batch_of(j)][:, (h % BATCH) * D : (h % BATCH + 1) * D],
+                    lhsT=e_codes[j][:, lane * P : (lane + 1) * P].bitcast(FP8X4),
+                    lhsT_scale=e_scales[j][:, lane * P : (lane + 1) * P],
+                    rhs=v_codes[half][:, h * D : (h + 1) * D].bitcast(FP8X4),
+                    rhs_scale=v_scales[half][:, h * D : (h + 1) * D],
+                    start=(lane == 0 or not one_head),
+                    stop=(lane == LANES - 1 or not one_head),
                 )
 
-        def regroup_v(w, h):
-            v_grouped[w, h] = work.tile([P, D, PACK], BF16, align_bytes=64, name="v_grouped")
+        def regroup_v(w, heads):
+            cols = slice(heads[0] * D, (heads[-1] + 1) * D)
+            v_grouped[w, heads] = work.tile([P, len(heads) * D, PACK], BF16, align_bytes=64, name="v_grouped")
             nc.vector.tensor_copy(
-                out=v_grouped[w, h][:].rearrange("p (c i) j -> p c j i", i=4),
-                in_=v_rows[w][:, :, h * D : (h + 1) * D].rearrange("p j (c i) -> p c j i", i=4),
+                out=v_grouped[w, heads][:].rearrange("p (c i) j -> p c j i", i=4),
+                in_=v_rows[w][:, :, cols].rearrange("p j (c i) -> p c j i", i=4),
             )
 
-        def quantise_v(w, h):
+        def quantise_v(w, heads):
+            cols = slice(heads[0] * D, (heads[-1] + 1) * D)
             nc.vector.quantize_mx(
-                out=v_codes[w][:, h * D : (h + 1) * D].bitcast(FP8X4),
-                scales=v_scales[w][:, h * D : (h + 1) * D],
-                in_=v_grouped[w, h][:].rearrange("p c j -> p (c j)"),
+                out=v_codes[w][:, cols].bitcast(FP8X4),
+                scales=v_scales[w][:, cols],
+                in_=v_grouped[w, heads][:].rearrange("p c j -> p (c j)"),
             )
 
         def enter_ring(b):
@@ -257,16 +291,12 @@ def tile_sparseselfattention_pa_kernel(tc, q_rot, k_rot, v, out):
                 out=v_scales[half][rows, :].bitcast(I32), in_=v_scales[b // HALF][rows, :].bitcast(I32)
             )
 
-        def sum_rows(batch):
-            totals[batch] = small.tile([P, BATCH], F32, name="totals")
-            nc.vector.tensor_reduce(out=totals[batch][:], in_=row_sums[batch][:], axis=AXIS_X, op=ALU.add)
-
         def invert_sums(batch):
             inverse[batch] = small.tile([P, BATCH], F32, name="inverse")
-            nc.vector.reciprocal(out=inverse[batch][:], in_=totals[batch][:])
+            nc.vector.reciprocal(out=inverse[batch][:], in_=row_sums[batch][:])
 
         def divide_and_store(batch):
-            g, first_head = units[batch * BATCH]
+            g, part = batch
             result = work.tile([P, BATCH, D], F32, name="result")
             nc.vector.tensor_tensor(
                 out=result[:],
@@ -275,36 +305,18 @@ def tile_sparseselfattention_pa_kernel(tc, q_rot, k_rot, v, out):
                 op=ALU.mult,
             )
             nc.sync.dma_start(
-                out=out2d[g * P : (g + 1) * P, first_head * D : (first_head + BATCH) * D],
+                out=out2d[g * P : (g + 1) * P, part * BATCH * D : (part + 1) * BATCH * D],
                 in_=result[:].rearrange("q h d -> q (h d)"),
             )
-
-        def is_unit(j):
-            return 0 <= j < len(units)
 
         turn_q(0)
         turn_k(0)
         for j in range(len(units) + LAG_STORE + 1):
-            closing = (j - LAG_STORE) // BATCH if is_unit(j - LAG_STORE) and (j - LAG_STORE) % BATCH == BATCH - 1 else None
-            window = None
-            if is_unit(j) and (units[j][0] == 0 or (units[j][0] + 2) % HALF == 0) and (units[j][0] + 2) // HALF < WINDOWS:
-                window = (units[j][0] + 2) // HALF
-
             if is_unit(j):
                 scores(j)
-                row_maximum(j, 0)
-            if closing is not None:
-                sum_rows(closing)
-            if window is not None:
-                regroup_v(window, units[j][1])
-            if is_unit(j):
-                row_maximum(j, 1)
-            if closing is not None:
-                invert_sums(closing)
+                negate_and_minimum(j)
             if is_unit(j - LAG_QUANT):
                 quantise_e(j - LAG_QUANT)
-            if window is not None:
-                quantise_v(window, units[j][1])
             if is_unit(j):
                 exp_bias(j)
             if is_unit(j - LAG_EXP):
@@ -314,12 +326,18 @@ def tile_sparseselfattention_pa_kernel(tc, q_rot, k_rot, v, out):
             if is_unit(j - LAG_TURN):
                 turn_e(j - LAG_TURN)
                 regroup_e(j - LAG_TURN)
-            if is_unit(j + 1 - LAG_PV) and units[j + 1 - LAG_PV][0] >= RING and units[j + 1 - LAG_PV][1] == 0:
+            if window_of(j) is not None:
+                regroup_v(window_of(j), units[j][1])
+            if ends_batch(j - LAG_TURN):
+                invert_sums(batch_of(j - LAG_TURN))
+            if window_of(j - 1) is not None:
+                quantise_v(window_of(j - 1), units[j - 1][1])
+            if is_unit(j + 1 - LAG_PV) and units[j + 1 - LAG_PV][0] >= RING and units[j + 1 - LAG_PV][1][0] == 0:
                 enter_ring(units[j + 1 - LAG_PV][0])
-            if closing is not None:
-                divide_and_store(closing)
+            if ends_batch(j - LAG_STORE):
+                divide_and_store(batch_of(j - LAG_STORE))
             if is_unit(j) and units[j][0] + 1 < GROUPS:
-                if units[j][1] == 1:
+                if 1 in units[j][1]:
                     turn_q(units[j][0] + 1)
-                if units[j][1] == 3:
+                if 3 in units[j][1]:
                     turn_k(units[j][0] + 1)

@@ -142,7 +142,6 @@ def tile_sparseselfattention_pa_kernel(tc, q_rot, k_rot, v, out):
         widths = {}
         negated = {}
         minima = {}
-        bias = {}
         row_sums = {}
         e_turned = {}
         e_grouped = {}
@@ -160,7 +159,7 @@ def tile_sparseselfattention_pa_kernel(tc, q_rot, k_rot, v, out):
             for h in range(H):
                 nc.tensor.transpose(bank[:, h, :], q_rows[g][:, h * D : (h + 1) * D], ident_bf[:])
             q_turned[g] = turned.tile([P, H, P], BF16, name="qT")
-            nc.vector.tensor_copy(out=q_turned[g][:], in_=bank[:])
+            nc.scalar.copy(out=q_turned[g][:], in_=bank[:])
 
         def turn_k(b):
             bank = turn_banks.tile([P, H, P], BF16, tag="turn", name="k_bank")
@@ -189,23 +188,17 @@ def tile_sparseselfattention_pa_kernel(tc, q_rot, k_rot, v, out):
                 banks[j].append(bank)
                 widths[j].append(len(live_slots(g, half)) * P)
 
-        def negate_and_minimum(j):
-            negated[j] = work.tile([P, LANES * K_PASS], F32, name="negated", bufs=4)
-            minima[j] = small.tile([P, LANES], F32, name="minima")
-            for lane in range(LANES):
-                nc.vector.tensor_scalar(
-                    out=negated[j][:, lane * K_PASS : lane * K_PASS + widths[j][lane]],
-                    in0=banks[j][lane][:, : widths[j][lane]],
-                    scalar1=-NORM, scalar2=None, op0=ALU.mult, op1=ALU.min,
-                    accum_out=minima[j][:, lane : lane + 1],
-                )
-
-        def exp_bias(j):
-            if len(units[j][1]) == 1:
-                bias[j] = small.tile([P, 1], F32, name="bias")
-                nc.vector.tensor_tensor(
-                    out=bias[j][:], in0=minima[j][:, 0:1], in1=minima[j][:, 1:2], op=ALU.min
-                )
+        def negate_and_minimum(j, lane):
+            if lane == 0:
+                negated[j] = work.tile([P, LANES * K_PASS], F32, name="negated", bufs=4)
+                minima[j] = small.tile([P, LANES], F32, name="minima")
+            carried = minima[j][:, 0:1] if lane == 1 and len(units[j][1]) == 1 else None
+            nc.vector.tensor_scalar(
+                out=negated[j][:, lane * K_PASS : lane * K_PASS + widths[j][lane]],
+                in0=banks[j][lane][:, : widths[j][lane]],
+                scalar1=-NORM, scalar2=carried, op0=ALU.mult, op1=ALU.min,
+                accum_out=minima[j][:, lane : lane + 1],
+            )
 
         def exponentials(j):
             heads = units[j][1]
@@ -216,7 +209,7 @@ def tile_sparseselfattention_pa_kernel(tc, q_rot, k_rot, v, out):
                 width = K_PASS + widths[j][1]
                 nc.scalar.activation(
                     out=e_tile(j)[:, :width], in_=negated[j][:, :width], func=ACT.Exp,
-                    bias=bias[j][:, 0:1], scale=-1.0,
+                    bias=minima[j][:, 1:2], scale=-1.0,
                     accum_out=sums[:, heads[0] % BATCH : heads[0] % BATCH + 1],
                 )
             else:
@@ -314,11 +307,11 @@ def tile_sparseselfattention_pa_kernel(tc, q_rot, k_rot, v, out):
         for j in range(len(units) + LAG_STORE + 1):
             if is_unit(j):
                 scores(j)
-                negate_and_minimum(j)
+                negate_and_minimum(j, 0)
             if is_unit(j - LAG_QUANT):
                 quantise_e(j - LAG_QUANT)
             if is_unit(j):
-                exp_bias(j)
+                negate_and_minimum(j, 1)
             if is_unit(j - LAG_EXP):
                 exponentials(j - LAG_EXP)
             if is_unit(j - LAG_PV):

@@ -109,6 +109,10 @@ def tile_sparseselfattention_pa_kernel(tc, q_rot, k_rot, v, out):
                     in_=v2d[w * K_PASS : (w + 1) * K_PASS, :].rearrange("(p j) c -> p j c", j=PACK),
                 )
 
+        warm = const.tile([P, 1], F32)
+        nc.vector.memset(warm[:], 0.0)
+        nc.scalar.activation(out=warm[:], in_=warm[:], func=ACT.Exp)
+
         ident_bf = const.tile([P, P], BF16)
         make_identity(nc, ident_bf[:])
         ident_f32 = const.tile([P, P], F32)
@@ -260,10 +264,12 @@ def tile_sparseselfattention_pa_kernel(tc, q_rot, k_rot, v, out):
 
         def regroup_v(w, heads):
             cols = slice(heads[0] * D, (heads[-1] + 1) * D)
-            v_grouped[w, heads] = work.tile([P, len(heads) * D, PACK], BF16, align_bytes=64, name="v_grouped")
-            nc.vector.tensor_copy(
-                out=v_grouped[w, heads][:].rearrange("p (c i) j -> p c j i", i=4),
-                in_=v_rows[w][:, :, cols].rearrange("p j (c i) -> p c j i", i=4),
+            v_grouped[w, heads] = work.tile(
+                [P, len(heads) * D, PACK], BF16, align_bytes=64, name="v_grouped", bufs=1
+            )
+            nc.gpsimd.tensor_scalar(
+                out=v_grouped[w, heads][:], in0=v_rows[w][:, :, cols].rearrange("p j c -> p c j"),
+                scalar1=1.0, scalar2=0.0, op0=ALU.mult, op1=ALU.add,
             )
 
         def quantise_v(w, heads):
@@ -310,6 +316,10 @@ def tile_sparseselfattention_pa_kernel(tc, q_rot, k_rot, v, out):
                 negate_and_minimum(j, 0)
             if is_unit(j - LAG_QUANT):
                 quantise_e(j - LAG_QUANT)
+            if window_of(j - 1) is not None:
+                quantise_v(window_of(j - 1), units[j - 1][1])
+            if window_of(j) is not None:
+                regroup_v(window_of(j), units[j][1])
             if is_unit(j):
                 negate_and_minimum(j, 1)
             if is_unit(j - LAG_EXP):
@@ -319,12 +329,8 @@ def tile_sparseselfattention_pa_kernel(tc, q_rot, k_rot, v, out):
             if is_unit(j - LAG_TURN):
                 turn_e(j - LAG_TURN)
                 regroup_e(j - LAG_TURN)
-            if window_of(j) is not None:
-                regroup_v(window_of(j), units[j][1])
             if ends_batch(j - LAG_TURN):
                 invert_sums(batch_of(j - LAG_TURN))
-            if window_of(j - 1) is not None:
-                quantise_v(window_of(j - 1), units[j - 1][1])
             if is_unit(j + 1 - LAG_PV) and units[j + 1 - LAG_PV][0] >= RING and units[j + 1 - LAG_PV][1][0] == 0:
                 enter_ring(units[j + 1 - LAG_PV][0])
             if ends_batch(j - LAG_STORE):

@@ -22,6 +22,8 @@ RING = 8
 HALF = 4
 K_PASS = HALF * P
 LANES = 2
+PLANES = 2
+PAIR = 2
 BATCH = 4
 WINDOWS = S // K_PASS
 NORM = 1.0 / (D**0.5)
@@ -89,8 +91,8 @@ def tile_sparseselfattention_pa_kernel(tc, q_rot, k_rot, v, out):
         turned = ctx.enter_context(tc.tile_pool(name="turned", bufs=2))
         work = ctx.enter_context(tc.tile_pool(name="work", bufs=3))
         small = ctx.enter_context(tc.tile_pool(name="small", bufs=4))
-        score_banks = ctx.enter_context(tc.psum_pool(name="score_banks", bufs=4))
-        turn_banks = ctx.enter_context(tc.psum_pool(name="turn_banks", bufs=2))
+        score_banks = ctx.enter_context(tc.psum_pool(name="score_banks", bufs=3))
+        turn_banks = ctx.enter_context(tc.psum_pool(name="turn_banks", bufs=3))
         ctx_banks = ctx.enter_context(tc.psum_pool(name="ctx_banks", bufs=2))
         ctx.enter_context(tc.manual_schedule())
 
@@ -155,6 +157,9 @@ def tile_sparseselfattention_pa_kernel(tc, q_rot, k_rot, v, out):
         v_grouped = {}
         inverse = {}
 
+        def by_plane(tile):
+            return tile[:].rearrange("q (u l p e) -> q u l p e", u=PLANES, l=LANES, e=PAIR)
+
         def e_tile(j):
             return e_tiles[len(units[j][1]), j % E_BUFFERS]
 
@@ -198,8 +203,8 @@ def tile_sparseselfattention_pa_kernel(tc, q_rot, k_rot, v, out):
                 minima[j] = small.tile([P, LANES], F32, name="minima")
             carried = minima[j][:, 0:1] if lane == 1 and len(units[j][1]) == 1 else None
             nc.vector.tensor_scalar(
-                out=negated[j][:, lane * K_PASS : lane * K_PASS + widths[j][lane]],
-                in0=banks[j][lane][:, : widths[j][lane]],
+                out=by_plane(negated[j])[:, :, lane, : widths[j][lane] // PACK, :].rearrange("q u p e -> q p u e"),
+                in0=banks[j][lane][:, : widths[j][lane]].rearrange("q (p u e) -> q p u e", u=PLANES, e=PAIR),
                 scalar1=-NORM, scalar2=carried, op0=ALU.mult, op1=ALU.min,
                 accum_out=minima[j][:, lane : lane + 1],
             )
@@ -210,32 +215,34 @@ def tile_sparseselfattention_pa_kernel(tc, q_rot, k_rot, v, out):
                 row_sums[batch_of(j)] = small.tile([P, BATCH], F32, name="row_sums")
             sums = row_sums[batch_of(j)]
             if len(heads) == 1:
-                width = K_PASS + widths[j][1]
+                run = (K_PASS + widths[j][1]) // PLANES
                 nc.scalar.activation(
-                    out=e_tile(j)[:, :width], in_=negated[j][:, :width], func=ACT.Exp,
-                    bias=minima[j][:, 1:2], scale=-1.0,
+                    out=e_tile(j)[:].rearrange("q (u x) -> q u x", u=PLANES)[:, :, :run],
+                    in_=negated[j][:].rearrange("q (u x) -> q u x", u=PLANES)[:, :, :run],
+                    func=ACT.Exp, bias=minima[j][:, 1:2], scale=-1.0,
                     accum_out=sums[:, heads[0] % BATCH : heads[0] % BATCH + 1],
                 )
             else:
                 for lane in range(LANES):
-                    cols = slice(lane * K_PASS, lane * K_PASS + widths[j][lane])
+                    run = widths[j][lane] // PLANES
                     nc.scalar.activation(
-                        out=e_tile(j)[:, cols], in_=negated[j][:, cols], func=ACT.Exp,
-                        bias=minima[j][:, lane : lane + 1], scale=-1.0,
+                        out=e_tile(j)[:].rearrange("q (u l x) -> q u l x", u=PLANES, l=LANES)[:, :, lane, :run],
+                        in_=negated[j][:].rearrange("q (u l x) -> q u l x", u=PLANES, l=LANES)[:, :, lane, :run],
+                        func=ACT.Exp, bias=minima[j][:, lane : lane + 1], scale=-1.0,
                         accum_out=sums[:, heads[lane] % BATCH : heads[lane] % BATCH + 1],
                     )
 
         def turn_e(j):
-            e_turned[j] = turn_banks.tile([P, LANES, 2, P], F32, tag="turn", name="e_turned")
-            words = e_tile(j)[:].bitcast(F32).rearrange("q (l p u) -> q l u p", l=LANES, u=2)
+            e_turned[j] = turn_banks.tile([P, LANES, PLANES, P], F32, tag="turn", name="e_turned")
+            words = e_tile(j)[:].bitcast(F32).rearrange("q (u l p) -> q u l p", u=PLANES, l=LANES)
             for lane in range(LANES):
-                for u in range(2):
-                    nc.tensor.transpose(e_turned[j][:, lane, u, :], words[:, lane, u, :], ident_f32[:])
+                for u in range(PLANES):
+                    nc.tensor.transpose(e_turned[j][:, lane, u, :], words[:, u, lane, :], ident_f32[:])
 
         def regroup_e(j):
             e_grouped[j] = work.tile([P, LANES * P * PACK], BF16, align_bytes=64, name="e_grouped")
             nc.scalar.copy(
-                out=e_grouped[j][:].bitcast(F32).rearrange("p (l q u) -> p l q u", l=LANES, u=2),
+                out=e_grouped[j][:].bitcast(F32).rearrange("p (l q u) -> p l q u", l=LANES, u=PLANES),
                 in_=e_turned[j][:].rearrange("p l u q -> p l q u"),
             )
 

@@ -203,8 +203,8 @@ def tile_sparseselfattention_pa_kernel(tc, q_rot, k_rot, v, out):
                 minima[j] = small.tile([P, LANES], F32, name="minima")
             carried = minima[j][:, 0:1] if lane == 1 and len(units[j][1]) == 1 else None
             nc.vector.tensor_scalar(
-                out=by_plane(negated[j])[:, :, lane, : widths[j][lane] // PACK, :].rearrange("q u p e -> q p u e"),
-                in0=banks[j][lane][:, : widths[j][lane]].rearrange("q (p u e) -> q p u e", u=PLANES, e=PAIR),
+                out=by_plane(negated[j])[:, :, lane, : widths[j][lane] // PACK, :],
+                in0=banks[j][lane][:, : widths[j][lane]].rearrange("q (p u e) -> q u p e", u=PLANES, e=PAIR),
                 scalar1=-NORM, scalar2=carried, op0=ALU.mult, op1=ALU.min,
                 accum_out=minima[j][:, lane : lane + 1],
             )

@@ -156,6 +156,7 @@ def tile_sparseselfattention_pa_kernel(tc, q_rot, k_rot, v, out):
         ctx_bank = {}
         v_grouped = {}
         inverse = {}
+        v_mixed = {}
 
         def by_plane(tile):
             return tile[:].rearrange("q (u l p e) -> q u l p e", u=PLANES, l=LANES, e=PAIR)
@@ -259,12 +260,13 @@ def tile_sparseselfattention_pa_kernel(tc, q_rot, k_rot, v, out):
                 ctx_bank[batch_of(j)] = ctx_banks.tile([P, BATCH * D], F32, name="ctx_bank")
             for lane in range(LANES):
                 h, half = lanes[j][lane]
+                codes, scales = v_operand(units[j][0], half)
                 nc.tensor.matmul_mx(
                     out=ctx_bank[batch_of(j)][:, (h % BATCH) * D : (h % BATCH + 1) * D],
                     lhsT=e_codes[j][:, lane * P : (lane + 1) * P].bitcast(FP8X4),
                     lhsT_scale=e_scales[j][:, lane * P : (lane + 1) * P],
-                    rhs=v_codes[half][:, h * D : (h + 1) * D].bitcast(FP8X4),
-                    rhs_scale=v_scales[half][:, h * D : (h + 1) * D],
+                    rhs=codes[:, h * D : (h + 1) * D].bitcast(FP8X4),
+                    rhs_scale=scales[:, h * D : (h + 1) * D],
                     start=(lane == 0 or not one_head),
                     stop=(lane == LANES - 1 or not one_head),
                 )
@@ -287,15 +289,25 @@ def tile_sparseselfattention_pa_kernel(tc, q_rot, k_rot, v, out):
                 in_=v_grouped[w, heads][:].rearrange("p c j -> p (c j)"),
             )
 
-        def enter_ring(b):
-            rows = slice((b % HALF) * 32, (b % HALF) * 32 + 32)
-            half = (b // HALF) % 2
-            nc.vector.tensor_copy(
-                out=v_codes[half][rows, :].bitcast(I32), in_=v_codes[b // HALF][rows, :].bitcast(I32)
-            )
-            nc.vector.tensor_copy(
-                out=v_scales[half][rows, :].bitcast(I32), in_=v_scales[b // HALF][rows, :].bitcast(I32)
-            )
+        def newest_window(g, half):
+            blocks = [ring_block(g, s) for s in range(half * HALF, (half + 1) * HALF)]
+            w = max(blocks) // HALF
+            return w, len([b for b in blocks if b // HALF == w])
+
+        def v_operand(g, half):
+            w, fresh = newest_window(g, half)
+            if w < LANES or fresh == HALF:
+                return v_codes[w], v_scales[w]
+            return v_mixed[w, fresh]
+
+        def mix_windows(w):
+            for fresh in range(1, HALF):
+                codes = const.tile([P, H * D], U32, align_bytes=64, name="mix_codes_%d_%d" % (w, fresh))
+                scales = const.tile([P, H * D], U8, align_bytes=64, name="mix_scales_%d_%d" % (w, fresh))
+                v_mixed[w, fresh] = (codes, scales)
+                for src, rows in ((w, slice(0, 32 * fresh)), (w - LANES, slice(32 * fresh, P))):
+                    nc.sync.dma_start(out=codes[rows, :].bitcast(I32), in_=v_codes[src][rows, :].bitcast(I32))
+                    nc.sync.dma_start(out=scales[rows, :].bitcast(I32), in_=v_scales[src][rows, :].bitcast(I32))
 
         def invert_sums(batch):
             inverse[batch] = small.tile([P, BATCH], F32, name="inverse")
@@ -338,8 +350,8 @@ def tile_sparseselfattention_pa_kernel(tc, q_rot, k_rot, v, out):
                 regroup_e(j - LAG_TURN)
             if ends_batch(j - LAG_TURN):
                 invert_sums(batch_of(j - LAG_TURN))
-            if is_unit(j + 1 - LAG_PV) and units[j + 1 - LAG_PV][0] >= RING and units[j + 1 - LAG_PV][1][0] == 0:
-                enter_ring(units[j + 1 - LAG_PV][0])
+            if window_of(j - 1) is not None and window_of(j - 1) >= LANES and H - 1 in units[j - 1][1]:
+                mix_windows(window_of(j - 1))
             if ends_batch(j - LAG_STORE):
                 divide_and_store(batch_of(j - LAG_STORE))
             if is_unit(j) and units[j][0] + 1 < GROUPS:

@@ -28,13 +28,13 @@ BATCH = 4
 WINDOWS = S // K_PASS
 NORM = 1.0 / (D**0.5)
 MASKED = -1.0e10
-E_BUFFERS = 3
+E_BUFFERS = 6
+MINUS_ONE = -1.0
 
-LAG_EXP = 1
 LAG_TURN = 2
 LAG_QUANT = 3
+LAG_INVERT = 3
 LAG_PV = 4
-LAG_STORE = 5
 
 FLOPS = 2 * 2 * H * P * D * (4 * K_PASS + 12 * 2 * K_PASS)
 
@@ -78,13 +78,16 @@ def tile_sparseselfattention_pa_kernel(tc, q_rot, k_rot, v, out):
     def ends_batch(j):
         return is_unit(j) and units[j][1][-1] % BATCH == BATCH - 1
 
-    def window_of(j):
-        if not is_unit(j):
-            return None
-        g = units[j][0]
-        if (g == 0 or (g + 2) % HALF == 0) and (g + 2) // HALF < WINDOWS:
-            return (g + 2) // HALF
-        return None
+    pairs = len(units) // 2
+
+    def is_pair(i):
+        return 0 <= i < pairs
+
+    v_steps = {}
+    for w in range(WINDOWS):
+        first = w * H // 2 if w < LANES else units.index((w * HALF - 2, (0,))) // 2
+        for n in range(H // 2):
+            v_steps[first + n] = (w, (2 * n, 2 * n + 1))
 
     with ExitStack() as ctx:
         const = ctx.enter_context(tc.tile_pool(name="const", bufs=1))
@@ -133,11 +136,16 @@ def tile_sparseselfattention_pa_kernel(tc, q_rot, k_rot, v, out):
         causal_bf = const.tile([P, P], BF16)
         nc.vector.tensor_copy(out=causal_bf[:], in_=causal_f32[:])
 
+        minus_one = const.tile([P, BATCH], F32)
+        nc.gpsimd.memset(minus_one[:], MINUS_ONE)
+
         e_tiles = {}
-        for heads in (1, 2):
-            for i in range(E_BUFFERS):
+        for i in range(E_BUFFERS):
+            for heads in (1, 2):
                 e_tiles[heads, i] = const.tile([P, LANES * K_PASS], BF16, name="e_%d_%d" % (heads, i))
-                nc.vector.memset(e_tiles[heads, i][:], 0.0)
+            nc.vector.memset(e_tiles[2, i][:], 0.0)
+            words = e_tiles[1, i][:].bitcast(F32).rearrange("q (u x) -> q u x", u=PLANES)
+            nc.gpsimd.memset(words[:, :, P + P // HALF :], 0.0)
 
         v_codes = [const.tile([P, H * D], U32, align_bytes=64, name="v_codes_%d" % w) for w in range(WINDOWS)]
         v_scales = [const.tile([P, H * D], U8, align_bytes=64, name="v_scales_%d" % w) for w in range(WINDOWS)]
@@ -178,25 +186,23 @@ def tile_sparseselfattention_pa_kernel(tc, q_rot, k_rot, v, out):
             k_turned[b] = turned.tile([P, H, P], BF16, name="kT", bufs=RING + 2)
             nc.scalar.copy(out=k_turned[b][:], in_=bank[:])
 
-        def scores(j):
+        def scores(j, lane):
             g = units[j][0]
-            banks[j] = []
-            widths[j] = []
-            for h, half in lanes[j]:
-                bank = score_banks.tile([P, K_PASS], F32, name="score_bank")
-                for s in live_slots(g, half):
-                    b = ring_block(g, s)
-                    cols = slice((s % HALF) * P, (s % HALF + 1) * P)
+            h, half = lanes[j][lane]
+            bank = score_banks.tile([P, K_PASS], F32, name="score_bank")
+            for s in live_slots(g, half):
+                b = ring_block(g, s)
+                cols = slice((s % HALF) * P, (s % HALF + 1) * P)
+                nc.tensor.matmul(
+                    bank[:, cols], lhsT=q_turned[g][:, h, :], rhs=k_turned[b][:, h, :],
+                    start=True, stop=(b != g),
+                )
+                if b == g:
                     nc.tensor.matmul(
-                        bank[:, cols], lhsT=q_turned[g][:, h, :], rhs=k_turned[b][:, h, :],
-                        start=True, stop=(b != g),
+                        bank[:, cols], lhsT=ident_bf[:], rhs=causal_bf[:], start=False, stop=True
                     )
-                    if b == g:
-                        nc.tensor.matmul(
-                            bank[:, cols], lhsT=ident_bf[:], rhs=causal_bf[:], start=False, stop=True
-                        )
-                banks[j].append(bank)
-                widths[j].append(len(live_slots(g, half)) * P)
+            banks[j, lane] = bank
+            widths[j, lane] = len(live_slots(g, half)) * P
 
         def negate_and_minimum(j, lane):
             if lane == 0:
@@ -204,8 +210,8 @@ def tile_sparseselfattention_pa_kernel(tc, q_rot, k_rot, v, out):
                 minima[j] = small.tile([P, LANES], F32, name="minima")
             carried = minima[j][:, 0:1] if lane == 1 and len(units[j][1]) == 1 else None
             nc.vector.tensor_scalar(
-                out=by_plane(negated[j])[:, :, lane, : widths[j][lane] // PACK, :],
-                in0=banks[j][lane][:, : widths[j][lane]].rearrange("q (p u e) -> q u p e", u=PLANES, e=PAIR),
+                out=by_plane(negated[j])[:, :, lane, : widths[j, lane] // PACK, :],
+                in0=banks[j, lane][:, : widths[j, lane]].rearrange("q (p u e) -> q u p e", u=PLANES, e=PAIR),
                 scalar1=-NORM, scalar2=carried, op0=ALU.mult, op1=ALU.min,
                 accum_out=minima[j][:, lane : lane + 1],
             )
@@ -216,7 +222,7 @@ def tile_sparseselfattention_pa_kernel(tc, q_rot, k_rot, v, out):
                 row_sums[batch_of(j)] = small.tile([P, BATCH], F32, name="row_sums")
             sums = row_sums[batch_of(j)]
             if len(heads) == 1:
-                run = (K_PASS + widths[j][1]) // PLANES
+                run = (K_PASS + widths[j, 1]) // PLANES
                 nc.scalar.activation(
                     out=e_tile(j)[:].rearrange("q (u x) -> q u x", u=PLANES)[:, :, :run],
                     in_=negated[j][:].rearrange("q (u x) -> q u x", u=PLANES)[:, :, :run],
@@ -225,7 +231,7 @@ def tile_sparseselfattention_pa_kernel(tc, q_rot, k_rot, v, out):
                 )
             else:
                 for lane in range(LANES):
-                    run = widths[j][lane] // PLANES
+                    run = widths[j, lane] // PLANES
                     nc.scalar.activation(
                         out=e_tile(j)[:].rearrange("q (u l x) -> q u l x", u=PLANES, l=LANES)[:, :, lane, :run],
                         in_=negated[j][:].rearrange("q (u l x) -> q u l x", u=PLANES, l=LANES)[:, :, lane, :run],
@@ -241,17 +247,21 @@ def tile_sparseselfattention_pa_kernel(tc, q_rot, k_rot, v, out):
                     nc.tensor.transpose(e_turned[j][:, lane, u, :], words[:, u, lane, :], ident_f32[:])
 
         def regroup_e(j):
-            e_grouped[j] = work.tile([P, LANES * P * PACK], BF16, align_bytes=64, name="e_grouped")
+            width = LANES * P * PACK
+            if j % 2 == 0:
+                e_grouped[j // 2] = work.tile([P, 2 * width], BF16, align_bytes=64, name="e_grouped")
             nc.scalar.copy(
-                out=e_grouped[j][:].bitcast(F32).rearrange("p (l q u) -> p l q u", l=LANES, u=PLANES),
+                out=e_grouped[j // 2][:, j % 2 * width : (j % 2 + 1) * width]
+                .bitcast(F32)
+                .rearrange("p (l q u) -> p l q u", l=LANES, u=PLANES),
                 in_=e_turned[j][:].rearrange("p l u q -> p l q u"),
             )
 
-        def quantise_e(j):
-            e_codes[j] = work.tile([P, LANES * P], U32, align_bytes=64, name="e_codes")
-            e_scales[j] = work.tile([P, LANES * P], U8, align_bytes=64, name="e_scales")
+        def quantise_e(i):
+            e_codes[i] = work.tile([P, 2 * LANES * P], U32, align_bytes=64, name="e_codes")
+            e_scales[i] = work.tile([P, 2 * LANES * P], U8, align_bytes=64, name="e_scales")
             nc.vector.quantize_mx(
-                out=e_codes[j][:].bitcast(FP8X4), scales=e_scales[j][:], in_=e_grouped[j][:]
+                out=e_codes[i][:].bitcast(FP8X4), scales=e_scales[i][:], in_=e_grouped[i][:]
             )
 
         def e_times_v(j):
@@ -261,10 +271,11 @@ def tile_sparseselfattention_pa_kernel(tc, q_rot, k_rot, v, out):
             for lane in range(LANES):
                 h, half = lanes[j][lane]
                 codes, scales = v_operand(units[j][0], half)
+                e_cols = slice((j % 2 * LANES + lane) * P, (j % 2 * LANES + lane + 1) * P)
                 nc.tensor.matmul_mx(
                     out=ctx_bank[batch_of(j)][:, (h % BATCH) * D : (h % BATCH + 1) * D],
-                    lhsT=e_codes[j][:, lane * P : (lane + 1) * P].bitcast(FP8X4),
-                    lhsT_scale=e_scales[j][:, lane * P : (lane + 1) * P],
+                    lhsT=e_codes[j // 2][:, e_cols].bitcast(FP8X4),
+                    lhsT_scale=e_scales[j // 2][:, e_cols],
                     rhs=codes[:, h * D : (h + 1) * D].bitcast(FP8X4),
                     rhs_scale=scales[:, h * D : (h + 1) * D],
                     start=(lane == 0 or not one_head),
@@ -302,16 +313,16 @@ def tile_sparseselfattention_pa_kernel(tc, q_rot, k_rot, v, out):
 
         def mix_windows(w):
             for fresh in range(1, HALF):
-                codes = const.tile([P, H * D], U32, align_bytes=64, name="mix_codes_%d_%d" % (w, fresh))
-                scales = const.tile([P, H * D], U8, align_bytes=64, name="mix_scales_%d_%d" % (w, fresh))
+                codes = const.tile([P, H * D], U32, align_bytes=64, name="mix_codes_%d" % fresh)
+                scales = const.tile([P, H * D], U8, align_bytes=64, name="mix_scales_%d" % fresh)
                 v_mixed[w, fresh] = (codes, scales)
                 for src, rows in ((w, slice(0, 32 * fresh)), (w - LANES, slice(32 * fresh, P))):
                     nc.sync.dma_start(out=codes[rows, :].bitcast(I32), in_=v_codes[src][rows, :].bitcast(I32))
                     nc.sync.dma_start(out=scales[rows, :].bitcast(I32), in_=v_scales[src][rows, :].bitcast(I32))
 
         def invert_sums(batch):
-            inverse[batch] = small.tile([P, BATCH], F32, name="inverse")
-            nc.vector.reciprocal(out=inverse[batch][:], in_=row_sums[batch][:])
+            inverse[batch] = small.tile([P, BATCH], F32, name="inverse", bufs=1)
+            nc.gpsimd.tensor_tensor(out=inverse[batch][:], in0=row_sums[batch][:], in1=minus_one[:], op=ALU.pow)
 
         def divide_and_store(batch):
             g, part = batch
@@ -329,33 +340,46 @@ def tile_sparseselfattention_pa_kernel(tc, q_rot, k_rot, v, out):
 
         turn_q(0)
         turn_k(0)
-        for j in range(len(units) + LAG_STORE + 1):
-            if is_unit(j):
-                scores(j)
-                negate_and_minimum(j, 0)
-            if is_unit(j - LAG_QUANT):
-                quantise_e(j - LAG_QUANT)
-            if window_of(j - 1) is not None:
-                quantise_v(window_of(j - 1), units[j - 1][1])
-            if window_of(j) is not None:
-                regroup_v(window_of(j), units[j][1])
-            if is_unit(j):
-                negate_and_minimum(j, 1)
-            if is_unit(j - LAG_EXP):
-                exponentials(j - LAG_EXP)
-            if is_unit(j - LAG_PV):
-                e_times_v(j - LAG_PV)
-            if is_unit(j - LAG_TURN):
-                turn_e(j - LAG_TURN)
-                regroup_e(j - LAG_TURN)
-            if ends_batch(j - LAG_TURN):
-                invert_sums(batch_of(j - LAG_TURN))
-            if window_of(j - 1) is not None and window_of(j - 1) >= LANES and H - 1 in units[j - 1][1]:
-                mix_windows(window_of(j - 1))
-            if ends_batch(j - LAG_STORE):
-                divide_and_store(batch_of(j - LAG_STORE))
-            if is_unit(j) and units[j][0] + 1 < GROUPS:
-                if 1 in units[j][1]:
-                    turn_q(units[j][0] + 1)
-                if 3 in units[j][1]:
-                    turn_k(units[j][0] + 1)
+        for i in range(pairs + LAG_PV):
+            a, b = 2 * i, 2 * i + 1
+            if is_pair(i):
+                scores(a, 0)
+                negate_and_minimum(a, 0)
+            if is_pair(i - 1):
+                exponentials(b - 2)
+            if is_pair(i - LAG_TURN):
+                turn_e(a - 2 * LAG_TURN)
+                regroup_e(a - 2 * LAG_TURN)
+            if is_pair(i):
+                scores(b, 0)
+                negate_and_minimum(b, 0)
+            g, heads = units[a] if is_pair(i) else (GROUPS, ())
+            if g + 1 < GROUPS and 0 in heads:
+                turn_q(g + 1)
+            if is_pair(i):
+                scores(a, 1)
+                negate_and_minimum(a, 1)
+                exponentials(a)
+            if is_pair(i - LAG_TURN):
+                turn_e(b - 2 * LAG_TURN)
+                regroup_e(b - 2 * LAG_TURN)
+            if is_pair(i - LAG_QUANT):
+                quantise_e(i - LAG_QUANT)
+            if i - 1 in v_steps:
+                quantise_v(*v_steps[i - 1])
+            if i in v_steps:
+                regroup_v(*v_steps[i])
+            if is_pair(i - LAG_PV):
+                e_times_v(a - 2 * LAG_PV)
+                e_times_v(b - 2 * LAG_PV)
+            if is_pair(i):
+                scores(b, 1)
+                negate_and_minimum(b, 1)
+            if is_pair(i - LAG_PV) and ends_batch(b - 2 * LAG_PV):
+                divide_and_store(batch_of(b - 2 * LAG_PV))
+            if is_pair(i - LAG_INVERT) and ends_batch(b - 2 * LAG_INVERT):
+                invert_sums(batch_of(b - 2 * LAG_INVERT))
+            if g + 1 < GROUPS and (2 in heads if g >= HALF else 0 in heads):
+                turn_k(g + 1)
+            if g >= RING and g % HALF == 0 and 0 in heads:
+                mix_windows(g // HALF)

@@ -17,10 +17,12 @@ H = 8
 D = 128
 P = 128
 PACK = 4
+WORD = 4
 GROUPS = S // P
 RING = 8
 HALF = 4
 K_PASS = HALF * P
+QUADRANT = 32
 LANES = 2
 PLANES = 2
 PAIR = 2
@@ -28,12 +30,14 @@ BATCH = 4
 WINDOWS = S // K_PASS
 NORM = 1.0 / (D**0.5)
 MASKED = -1.0e10
-E_BUFFERS = 6
 MINUS_ONE = -1.0
+E_BUFFERS = 6
+
+ORDER = list(range(2, GROUPS)) + [1, 0]
+FIRST_GROUP = ORDER[0]
 
 LAG_TURN = 2
 LAG_QUANT = 3
-LAG_INVERT = 3
 LAG_PV = 4
 
 FLOPS = 2 * 2 * H * P * D * (4 * K_PASS + 12 * 2 * K_PASS)
@@ -43,8 +47,31 @@ def ring_block(g, slot):
     return g - (g - slot) % RING
 
 
-def live_slots(g, half):
-    return [s for s in range(half * HALF, (half + 1) * HALF) if ring_block(g, s) >= 0]
+def heads_of_lane(g):
+    return HALF // (g + 1) if g < HALF else 1
+
+
+def units_of(g):
+    if g >= HALF:
+        return [(g, (((h,), 0), ((h,), 1))) for h in range(H)]
+    n = heads_of_lane(g)
+    lanes = [(tuple(range(h, h + n)), 0) for h in range(0, H, n)]
+    return [(g, (lanes[i], lanes[i + 1])) for i in range(0, len(lanes), LANES)]
+
+
+def lane_blocks(g, lane):
+    heads, half = lane
+    if g < HALF:
+        return [(h, b, i * (g + 1) + b) for i, h in enumerate(heads) for b in range(g + 1)]
+    ring = [(ring_block(g, half * HALF + s), s) for s in range(HALF)]
+    return [(heads[0], b, s) for b, s in ring if b >= 0]
+
+
+def lane_pieces(g, lane):
+    slots = {}
+    for h, b, s in lane_blocks(g, lane):
+        slots.setdefault(h, []).append(s)
+    return [(h, min(ss) * P, len(ss) * P) for h, ss in slots.items()]
 
 
 def tile_sparseselfattention_pa_kernel(tc, q_rot, k_rot, v, out):
@@ -55,45 +82,38 @@ def tile_sparseselfattention_pa_kernel(tc, q_rot, k_rot, v, out):
     out2d = out.rearrange("s b c -> s (b c)")
 
     units = []
-    lanes = []
-    for g in range(GROUPS):
-        if g < HALF:
-            for h in range(0, H, LANES):
-                units.append((g, (h, h + 1)))
-                lanes.append(((h, 0), (h + 1, 0)))
-        else:
-            for h in range(H):
-                units.append((g, (h,)))
-                lanes.append(((h, 0), (h, 1)))
+    rounds = []
+    first_round = {}
+    last_round = {}
+    for g in ORDER:
+        of_group = units_of(g)
+        first_round[g] = len(rounds)
+        for n in range(0, len(of_group), 2):
+            pair = of_group[n : n + 2]
+            rounds.append(list(range(len(units), len(units) + len(pair))))
+            units.extend(pair)
+        last_round[g] = len(rounds) - 1
 
-    def is_unit(j):
-        return 0 <= j < len(units)
+    def unit(i, k):
+        return rounds[i][k] if 0 <= i < len(rounds) and k < len(rounds[i]) else None
 
-    def batch_of(j):
-        return (units[j][0], units[j][1][0] // BATCH)
+    def one_head(j):
+        return units[j][0] >= HALF
 
-    def opens_batch(j):
-        return units[j][1][0] % BATCH == 0
-
-    def ends_batch(j):
-        return is_unit(j) and units[j][1][-1] % BATCH == BATCH - 1
-
-    pairs = len(units) // 2
-
-    def is_pair(i):
-        return 0 <= i < pairs
+    def heads_of(j):
+        return sorted(set(h for heads, half in units[j][1] for h in heads))
 
     v_steps = {}
     for w in range(WINDOWS):
-        first = w * H // 2 if w < LANES else units.index((w * HALF - 2, (0,))) // 2
+        start = w * H // 2 if w < LANES else first_round[w * HALF - 2]
         for n in range(H // 2):
-            v_steps[first + n] = (w, (2 * n, 2 * n + 1))
+            v_steps[start + n] = (w, (2 * n, 2 * n + 1))
 
     with ExitStack() as ctx:
         const = ctx.enter_context(tc.tile_pool(name="const", bufs=1))
         turned = ctx.enter_context(tc.tile_pool(name="turned", bufs=2))
-        work = ctx.enter_context(tc.tile_pool(name="work", bufs=3))
-        small = ctx.enter_context(tc.tile_pool(name="small", bufs=4))
+        work = ctx.enter_context(tc.tile_pool(name="work", bufs=2))
+        small = ctx.enter_context(tc.tile_pool(name="small", bufs=6))
         score_banks = ctx.enter_context(tc.psum_pool(name="score_banks", bufs=3))
         turn_banks = ctx.enter_context(tc.psum_pool(name="turn_banks", bufs=3))
         ctx_banks = ctx.enter_context(tc.psum_pool(name="ctx_banks", bufs=2))
@@ -102,17 +122,26 @@ def tile_sparseselfattention_pa_kernel(tc, q_rot, k_rot, v, out):
         q_rows = {}
         k_rows = {}
         v_rows = {}
-        for g in range(GROUPS):
-            for name, src, rows in (("q", q2d, q_rows), ("k", k2d, k_rows)):
-                rows[g] = const.tile([P, H * D], BF16, name="%s_rows_%d" % (name, g))
-                nc.sync.dma_start(out=rows[g][:], in_=src[g * P : (g + 1) * P, :])
-            if g % 2 == 0 and g // 2 < WINDOWS:
-                w = g // 2
-                v_rows[w] = const.tile([P, PACK, H * D], BF16, name="v_rows_%d" % w)
-                nc.sync.dma_start(
-                    out=v_rows[w][:],
-                    in_=v2d[w * K_PASS : (w + 1) * K_PASS, :].rearrange("(p j) c -> p j c", j=PACK),
-                )
+
+        def load_rows(rows, src, name, g):
+            rows[g] = const.tile([P, H * D], BF16, name="%s_rows_%d" % (name, g))
+            nc.sync.dma_start(out=rows[g][:], in_=src[g * P : (g + 1) * P, :])
+
+        def load_window(w):
+            v_rows[w] = work.tile([P, PACK, H * D], BF16, name="v_rows", bufs=WINDOWS - 1)
+            nc.sync.dma_start(
+                out=v_rows[w][:],
+                in_=v2d[w * K_PASS : (w + 1) * K_PASS, :].rearrange("(p j) c -> p j c", j=PACK),
+            )
+
+        for g in ORDER:
+            load_rows(q_rows, q2d, "q", g)
+            for b in range(g + 1):
+                if b not in k_rows:
+                    load_rows(k_rows, k2d, "k", b)
+            if FIRST_GROUP < g < FIRST_GROUP + WINDOWS:
+                load_window(g - FIRST_GROUP - 1)
+        load_window(WINDOWS - 1)
 
         warm = const.tile([P, 1], F32)
         nc.vector.memset(warm[:], 0.0)
@@ -135,64 +164,75 @@ def tile_sparseselfattention_pa_kernel(tc, q_rot, k_rot, v, out):
         )
         causal_bf = const.tile([P, P], BF16)
         nc.vector.tensor_copy(out=causal_bf[:], in_=causal_f32[:])
-
-        minus_one = const.tile([P, BATCH], F32)
+        minus_one = const.tile([P, H], F32)
         nc.gpsimd.memset(minus_one[:], MINUS_ONE)
 
         e_tiles = {}
-        for i in range(E_BUFFERS):
-            for heads in (1, 2):
-                e_tiles[heads, i] = const.tile([P, LANES * K_PASS], BF16, name="e_%d_%d" % (heads, i))
-            nc.vector.memset(e_tiles[2, i][:], 0.0)
-            words = e_tiles[1, i][:].bitcast(F32).rearrange("q (u x) -> q u x", u=PLANES)
-            nc.gpsimd.memset(words[:, :, P + P // HALF :], 0.0)
+        for n in range(E_BUFFERS):
+            for one in (False, True):
+                e_tiles[one, n] = const.tile([P, LANES * K_PASS], BF16, name="e_%d_%d" % (one, n))
+            nc.vector.memset(e_tiles[False, n][:], 0.0)
+            words = e_tiles[True, n][:].bitcast(F32).rearrange("q (u x) -> q u x", u=PLANES)
+            nc.gpsimd.memset(words[:, :, P + QUADRANT :], 0.0)
 
-        v_codes = [const.tile([P, H * D], U32, align_bytes=64, name="v_codes_%d" % w) for w in range(WINDOWS)]
-        v_scales = [const.tile([P, H * D], U8, align_bytes=64, name="v_scales_%d" % w) for w in range(WINDOWS)]
+        def v_tiles(name):
+            return (
+                const.tile([P, H * D], U32, align_bytes=64, name="codes_" + name),
+                const.tile([P, H * D], U8, align_bytes=64, name="scales_" + name),
+            )
+
+        v_windows = [v_tiles("window_%d" % w) for w in range(WINDOWS)]
+        v_mixed = {}
+        v_shared = {}
+        for g in range(HALF):
+            if heads_of_lane(g) > 1:
+                v_shared[g] = v_tiles("shared_%d" % g)
+                for tile in v_shared[g]:
+                    nc.gpsimd.memset(tile[:].bitcast(I32), 0)
 
         q_turned = {}
         k_turned = {}
         banks = {}
-        widths = {}
         negated = {}
         minima = {}
+        lowest = {}
         row_sums = {}
+        inverse = {}
         e_turned = {}
         e_grouped = {}
         e_codes = {}
         e_scales = {}
         ctx_bank = {}
         v_grouped = {}
-        inverse = {}
-        v_mixed = {}
 
         def by_plane(tile):
             return tile[:].rearrange("q (u l p e) -> q u l p e", u=PLANES, l=LANES, e=PAIR)
 
         def e_tile(j):
-            return e_tiles[len(units[j][1]), j % E_BUFFERS]
+            return e_tiles[one_head(j), j % E_BUFFERS]
+
+        def turn(rows, out_tile):
+            bank = turn_banks.tile([P, H, P], BF16, tag="turn", name="rows_bank")
+            for h in range(H):
+                nc.tensor.transpose(bank[:, h, :], rows[:, h * D : (h + 1) * D], ident_bf[:])
+            nc.scalar.copy(out=out_tile[:], in_=bank[:])
 
         def turn_q(g):
-            bank = turn_banks.tile([P, H, P], BF16, tag="turn", name="q_bank")
-            for h in range(H):
-                nc.tensor.transpose(bank[:, h, :], q_rows[g][:, h * D : (h + 1) * D], ident_bf[:])
-            q_turned[g] = turned.tile([P, H, P], BF16, name="qT")
-            nc.scalar.copy(out=q_turned[g][:], in_=bank[:])
+            q_turned[g] = turned.tile([P, H, P], BF16, name="qT", bufs=3)
+            turn(q_rows[g], q_turned[g])
 
         def turn_k(b):
-            bank = turn_banks.tile([P, H, P], BF16, tag="turn", name="k_bank")
-            for h in range(H):
-                nc.tensor.transpose(bank[:, h, :], k_rows[b][:, h * D : (h + 1) * D], ident_bf[:])
-            k_turned[b] = turned.tile([P, H, P], BF16, name="kT", bufs=RING + 2)
-            nc.scalar.copy(out=k_turned[b][:], in_=bank[:])
+            if b < FIRST_GROUP:
+                k_turned[b] = const.tile([P, H, P], BF16, name="kT_%d" % b)
+            else:
+                k_turned[b] = turned.tile([P, H, P], BF16, name="kT", bufs=RING + 1)
+            turn(k_rows[b], k_turned[b])
 
         def scores(j, lane):
-            g = units[j][0]
-            h, half = lanes[j][lane]
+            g, lanes = units[j]
             bank = score_banks.tile([P, K_PASS], F32, name="score_bank")
-            for s in live_slots(g, half):
-                b = ring_block(g, s)
-                cols = slice((s % HALF) * P, (s % HALF + 1) * P)
+            for h, b, s in lane_blocks(g, lanes[lane]):
+                cols = slice(s * P, (s + 1) * P)
                 nc.tensor.matmul(
                     bank[:, cols], lhsT=q_turned[g][:, h, :], rhs=k_turned[b][:, h, :],
                     start=True, stop=(b != g),
@@ -202,41 +242,51 @@ def tile_sparseselfattention_pa_kernel(tc, q_rot, k_rot, v, out):
                         bank[:, cols], lhsT=ident_bf[:], rhs=causal_bf[:], start=False, stop=True
                     )
             banks[j, lane] = bank
-            widths[j, lane] = len(live_slots(g, half)) * P
 
         def negate_and_minimum(j, lane):
+            g, lanes = units[j]
             if lane == 0:
-                negated[j] = work.tile([P, LANES * K_PASS], F32, name="negated", bufs=4)
-                minima[j] = small.tile([P, LANES], F32, name="minima")
-            carried = minima[j][:, 0:1] if lane == 1 and len(units[j][1]) == 1 else None
-            nc.vector.tensor_scalar(
-                out=by_plane(negated[j])[:, :, lane, : widths[j, lane] // PACK, :],
-                in0=banks[j, lane][:, : widths[j, lane]].rearrange("q (p u e) -> q u p e", u=PLANES, e=PAIR),
-                scalar1=-NORM, scalar2=carried, op0=ALU.mult, op1=ALU.min,
-                accum_out=minima[j][:, lane : lane + 1],
-            )
+                negated[j] = work.tile([P, LANES * K_PASS], F32, name="negated", bufs=5)
+                minima[j] = small.tile([P, LANES * HALF], F32, name="minima")
+            for n, (h, first, width) in enumerate(lane_pieces(g, lanes[lane])):
+                column = lane * heads_of_lane(g) + n
+                nc.vector.tensor_scalar(
+                    out=by_plane(negated[j])[:, :, lane, first // PACK : (first + width) // PACK, :],
+                    in0=banks[j, lane][:, first : first + width].rearrange(
+                        "q (p u e) -> q u p e", u=PLANES, e=PAIR
+                    ),
+                    scalar1=-NORM, scalar2=None, op0=ALU.mult, op1=ALU.min,
+                    accum_out=minima[j][:, column : column + 1],
+                )
+            if one_head(j) and lane == LANES - 1:
+                lowest[j] = small.tile([P, 1], F32, name="lowest")
+                nc.gpsimd.tensor_scalar(
+                    out=lowest[j][:], in0=minima[j][:, 0:1], scalar1=minima[j][:, 1:2], scalar2=0.0,
+                    op0=ALU.min, op1=ALU.add,
+                )
 
         def exponentials(j):
-            heads = units[j][1]
-            if opens_batch(j):
-                row_sums[batch_of(j)] = small.tile([P, BATCH], F32, name="row_sums")
-            sums = row_sums[batch_of(j)]
-            if len(heads) == 1:
-                run = (K_PASS + widths[j, 1]) // PLANES
+            g, lanes = units[j]
+            if g not in row_sums:
+                row_sums[g] = small.tile([P, H], F32, name="row_sums")
+            if one_head(j):
+                h, first, width = lane_pieces(g, lanes[1])[0]
+                run = (K_PASS + width) // PLANES
                 nc.scalar.activation(
                     out=e_tile(j)[:].rearrange("q (u x) -> q u x", u=PLANES)[:, :, :run],
                     in_=negated[j][:].rearrange("q (u x) -> q u x", u=PLANES)[:, :, :run],
-                    func=ACT.Exp, bias=minima[j][:, 1:2], scale=-1.0,
-                    accum_out=sums[:, heads[0] % BATCH : heads[0] % BATCH + 1],
+                    func=ACT.Exp, bias=lowest[j][:], scale=-1.0, accum_out=row_sums[g][:, h : h + 1],
                 )
-            else:
-                for lane in range(LANES):
-                    run = widths[j, lane] // PLANES
+                return
+            for lane in range(LANES):
+                for n, (h, first, width) in enumerate(lane_pieces(g, lanes[lane])):
+                    column = lane * heads_of_lane(g) + n
+                    run = slice(first // PLANES, (first + width) // PLANES)
                     nc.scalar.activation(
-                        out=e_tile(j)[:].rearrange("q (u l x) -> q u l x", u=PLANES, l=LANES)[:, :, lane, :run],
-                        in_=negated[j][:].rearrange("q (u l x) -> q u l x", u=PLANES, l=LANES)[:, :, lane, :run],
-                        func=ACT.Exp, bias=minima[j][:, lane : lane + 1], scale=-1.0,
-                        accum_out=sums[:, heads[lane] % BATCH : heads[lane] % BATCH + 1],
+                        out=e_tile(j)[:].rearrange("q (u l x) -> q u l x", u=PLANES, l=LANES)[:, :, lane, run],
+                        in_=negated[j][:].rearrange("q (u l x) -> q u l x", u=PLANES, l=LANES)[:, :, lane, run],
+                        func=ACT.Exp, bias=minima[j][:, column : column + 1], scale=-1.0,
+                        accum_out=row_sums[g][:, h : h + 1],
                     )
 
         def turn_e(j):
@@ -246,40 +296,54 @@ def tile_sparseselfattention_pa_kernel(tc, q_rot, k_rot, v, out):
                 for u in range(PLANES):
                     nc.tensor.transpose(e_turned[j][:, lane, u, :], words[:, u, lane, :], ident_f32[:])
 
-        def regroup_e(j):
+        def regroup_e(i, k):
             width = LANES * P * PACK
-            if j % 2 == 0:
-                e_grouped[j // 2] = work.tile([P, 2 * width], BF16, align_bytes=64, name="e_grouped")
+            if k == 0:
+                e_grouped[i] = work.tile([P, 2 * width], BF16, align_bytes=64, name="e_grouped")
             nc.scalar.copy(
-                out=e_grouped[j // 2][:, j % 2 * width : (j % 2 + 1) * width]
+                out=e_grouped[i][:, k * width : (k + 1) * width]
                 .bitcast(F32)
                 .rearrange("p (l q u) -> p l q u", l=LANES, u=PLANES),
-                in_=e_turned[j][:].rearrange("p l u q -> p l q u"),
+                in_=e_turned[unit(i, k)][:].rearrange("p l u q -> p l q u"),
             )
 
         def quantise_e(i):
+            words = len(rounds[i]) * LANES * P
             e_codes[i] = work.tile([P, 2 * LANES * P], U32, align_bytes=64, name="e_codes")
             e_scales[i] = work.tile([P, 2 * LANES * P], U8, align_bytes=64, name="e_scales")
             nc.vector.quantize_mx(
-                out=e_codes[i][:].bitcast(FP8X4), scales=e_scales[i][:], in_=e_grouped[i][:]
+                out=e_codes[i][:, :words].bitcast(FP8X4),
+                scales=e_scales[i][:, :words],
+                in_=e_grouped[i][:, : words * PACK],
             )
 
-        def e_times_v(j):
-            one_head = len(units[j][1]) == 1
-            if opens_batch(j):
-                ctx_bank[batch_of(j)] = ctx_banks.tile([P, BATCH * D], F32, name="ctx_bank")
-            for lane in range(LANES):
-                h, half = lanes[j][lane]
-                codes, scales = v_operand(units[j][0], half)
-                e_cols = slice((j % 2 * LANES + lane) * P, (j % 2 * LANES + lane + 1) * P)
+        def v_operand(g, half):
+            if g in v_shared:
+                return v_shared[g]
+            blocks = [ring_block(g, half * HALF + s) for s in range(HALF)]
+            w = max(blocks) // HALF
+            fresh = len([b for b in blocks if b // HALF == w])
+            return v_windows[w] if w < LANES or fresh == HALF else v_mixed[w, fresh]
+
+        def e_times_v(i, k):
+            j = unit(i, k)
+            g, lanes = units[j]
+            for lane, (heads, half) in enumerate(lanes):
+                batch = (g, heads[0] // BATCH)
+                if batch not in ctx_bank:
+                    ctx_bank[batch] = ctx_banks.tile([P, BATCH * D], F32, name="ctx_bank")
+                codes, scales = v_operand(g, half)
+                e_cols = slice((k * LANES + lane) * P, (k * LANES + lane + 1) * P)
+                v_cols = slice(heads[0] * D, (heads[-1] + 1) * D)
+                first = heads[0] % BATCH
                 nc.tensor.matmul_mx(
-                    out=ctx_bank[batch_of(j)][:, (h % BATCH) * D : (h % BATCH + 1) * D],
-                    lhsT=e_codes[j // 2][:, e_cols].bitcast(FP8X4),
-                    lhsT_scale=e_scales[j // 2][:, e_cols],
-                    rhs=codes[:, h * D : (h + 1) * D].bitcast(FP8X4),
-                    rhs_scale=scales[:, h * D : (h + 1) * D],
-                    start=(lane == 0 or not one_head),
-                    stop=(lane == LANES - 1 or not one_head),
+                    out=ctx_bank[batch][:, first * D : (first + len(heads)) * D],
+                    lhsT=e_codes[i][:, e_cols].bitcast(FP8X4),
+                    lhsT_scale=e_scales[i][:, e_cols],
+                    rhs=codes[:, v_cols].bitcast(FP8X4),
+                    rhs_scale=scales[:, v_cols],
+                    start=(lane == 0 or not one_head(j)),
+                    stop=(lane == LANES - 1 or not one_head(j)),
                 )
 
         def regroup_v(w, heads):
@@ -294,43 +358,46 @@ def tile_sparseselfattention_pa_kernel(tc, q_rot, k_rot, v, out):
 
         def quantise_v(w, heads):
             cols = slice(heads[0] * D, (heads[-1] + 1) * D)
+            codes, scales = v_windows[w]
             nc.vector.quantize_mx(
-                out=v_codes[w][:, cols].bitcast(FP8X4),
-                scales=v_scales[w][:, cols],
+                out=codes[:, cols].bitcast(FP8X4),
+                scales=scales[:, cols],
                 in_=v_grouped[w, heads][:].rearrange("p c j -> p (c j)"),
             )
 
-        def newest_window(g, half):
-            blocks = [ring_block(g, s) for s in range(half * HALF, (half + 1) * HALF)]
-            w = max(blocks) // HALF
-            return w, len([b for b in blocks if b // HALF == w])
-
-        def v_operand(g, half):
-            w, fresh = newest_window(g, half)
-            if w < LANES or fresh == HALF:
-                return v_codes[w], v_scales[w]
-            return v_mixed[w, fresh]
-
         def mix_windows(w):
             for fresh in range(1, HALF):
-                codes = const.tile([P, H * D], U32, align_bytes=64, name="mix_codes_%d" % fresh)
-                scales = const.tile([P, H * D], U8, align_bytes=64, name="mix_scales_%d" % fresh)
-                v_mixed[w, fresh] = (codes, scales)
-                for src, rows in ((w, slice(0, 32 * fresh)), (w - LANES, slice(32 * fresh, P))):
-                    nc.sync.dma_start(out=codes[rows, :].bitcast(I32), in_=v_codes[src][rows, :].bitcast(I32))
-                    nc.sync.dma_start(out=scales[rows, :].bitcast(I32), in_=v_scales[src][rows, :].bitcast(I32))
+                v_mixed[w, fresh] = v_tiles("mixed_%d" % fresh)
+                for src, rows in ((w, slice(0, QUADRANT * fresh)), (w - LANES, slice(QUADRANT * fresh, P))):
+                    for to, of in zip(v_mixed[w, fresh], v_windows[src]):
+                        nc.sync.dma_start(out=to[rows, :].bitcast(I32), in_=of[rows, :].bitcast(I32))
 
-        def invert_sums(batch):
-            inverse[batch] = small.tile([P, BATCH], F32, name="inverse", bufs=1)
-            nc.gpsimd.tensor_tensor(out=inverse[batch][:], in0=row_sums[batch][:], in1=minus_one[:], op=ALU.pow)
+        def share_lanes():
+            for g, shared in v_shared.items():
+                n_heads = heads_of_lane(g)
+                rows = QUADRANT * (g + 1)
+                for n in range(n_heads):
+                    for to, of in zip(shared, v_windows[0]):
+                        nc.sync.dma_start(
+                            out=to[n * rows : (n + 1) * rows, :]
+                            .bitcast(I32)
+                            .rearrange("p (l n x) -> p l n x", l=H // n_heads, n=n_heads)[:, :, n, :],
+                            in_=of[0:rows, :]
+                            .bitcast(I32)
+                            .rearrange("p (l n x) -> p l n x", l=H // n_heads, n=n_heads)[:, :, n, :],
+                        )
 
-        def divide_and_store(batch):
-            g, part = batch
-            result = work.tile([P, BATCH, D], F32, name="result")
+        def invert_sums(g):
+            inverse[g] = small.tile([P, H], F32, name="inverse")
+            nc.gpsimd.tensor_tensor(out=inverse[g][:], in0=row_sums[g][:], in1=minus_one[:], op=ALU.pow)
+
+        def divide_and_store(g, part):
+            heads = slice(part * BATCH, (part + 1) * BATCH)
+            result = work.tile([P, BATCH, D], F32, name="result", bufs=3)
             nc.vector.tensor_tensor(
                 out=result[:],
-                in0=ctx_bank[batch][:].rearrange("q (h d) -> q h d", h=BATCH),
-                in1=inverse[batch][:].unsqueeze(2).to_broadcast([P, BATCH, D]),
+                in0=ctx_bank[g, part][:].rearrange("q (h d) -> q h d", h=BATCH),
+                in1=inverse[g][:, heads].unsqueeze(2).to_broadcast([P, BATCH, D]),
                 op=ALU.mult,
             )
             nc.sync.dma_start(
@@ -338,48 +405,70 @@ def tile_sparseselfattention_pa_kernel(tc, q_rot, k_rot, v, out):
                 in_=result[:].rearrange("q h d -> q (h d)"),
             )
 
-        turn_q(0)
-        turn_k(0)
-        for i in range(pairs + LAG_PV):
-            a, b = 2 * i, 2 * i + 1
-            if is_pair(i):
+        turns = {}
+        for g, following in zip(ORDER, ORDER[1:]):
+            start = first_round[g]
+            if following > g:
+                turns[start, 0] = (turn_q, following)
+                turns[(start + 1, 0) if g >= HALF else (start, 1)] = (turn_k, following)
+        for n, g in enumerate(ORDER[ORDER.index(GROUPS - 1) + 1 :]):
+            turns[first_round[GROUPS - 1] + n, 0] = (turn_q, g)
+
+        def turn_rows(i, place):
+            if (i, place) in turns:
+                call, g = turns[i, place]
+                call(g)
+
+        turn_q(FIRST_GROUP)
+        for b in range(FIRST_GROUP + 1):
+            turn_k(b)
+        for i in range(len(rounds) + LAG_PV):
+            a, b = unit(i, 0), unit(i, 1)
+            g = units[a][0] if a is not None else None
+            if a is not None:
                 scores(a, 0)
                 negate_and_minimum(a, 0)
-            if is_pair(i - 1):
-                exponentials(b - 2)
-            if is_pair(i - LAG_TURN):
-                turn_e(a - 2 * LAG_TURN)
-                regroup_e(a - 2 * LAG_TURN)
-            if is_pair(i):
-                scores(b, 0)
-                negate_and_minimum(b, 0)
-            g, heads = units[a] if is_pair(i) else (GROUPS, ())
-            if g + 1 < GROUPS and 0 in heads:
-                turn_q(g + 1)
-            if is_pair(i):
+            if unit(i - LAG_TURN, 0) is not None:
+                turn_e(unit(i - LAG_TURN, 0))
+                regroup_e(i - LAG_TURN, 0)
+            if unit(i - 1, 1) is not None:
+                exponentials(unit(i - 1, 1))
+            if a is not None:
                 scores(a, 1)
                 negate_and_minimum(a, 1)
-                exponentials(a)
-            if is_pair(i - LAG_TURN):
-                turn_e(b - 2 * LAG_TURN)
-                regroup_e(b - 2 * LAG_TURN)
-            if is_pair(i - LAG_QUANT):
+            turn_rows(i, 0)
+            if b is not None:
+                scores(b, 0)
+                negate_and_minimum(b, 0)
+            if unit(i - LAG_TURN, 1) is not None:
+                turn_e(unit(i - LAG_TURN, 1))
+                regroup_e(i - LAG_TURN, 1)
+            if unit(i - LAG_QUANT, 0) is not None:
                 quantise_e(i - LAG_QUANT)
             if i - 1 in v_steps:
                 quantise_v(*v_steps[i - 1])
             if i in v_steps:
                 regroup_v(*v_steps[i])
-            if is_pair(i - LAG_PV):
-                e_times_v(a - 2 * LAG_PV)
-                e_times_v(b - 2 * LAG_PV)
-            if is_pair(i):
+            if a is not None:
+                exponentials(a)
+            for k in range(2):
+                if unit(i - LAG_PV, k) is not None:
+                    e_times_v(i - LAG_PV, k)
+            if b is not None:
                 scores(b, 1)
                 negate_and_minimum(b, 1)
-            if is_pair(i - LAG_PV) and ends_batch(b - 2 * LAG_PV):
-                divide_and_store(batch_of(b - 2 * LAG_PV))
-            if is_pair(i - LAG_INVERT) and ends_batch(b - 2 * LAG_INVERT):
-                invert_sums(batch_of(b - 2 * LAG_INVERT))
-            if g + 1 < GROUPS and (2 in heads if g >= HALF else 0 in heads):
-                turn_k(g + 1)
-            if g >= RING and g % HALF == 0 and 0 in heads:
-                mix_windows(g // HALF)
+            for k in range(2):
+                j = unit(i - LAG_PV, k)
+                if j is not None:
+                    for h in heads_of(j):
+                        if h % BATCH == BATCH - 1:
+                            divide_and_store(units[j][0], h // BATCH)
+            for done in ORDER:
+                if last_round[done] == i - 1:
+                    invert_sums(done)
+            turn_rows(i, 1)
+            if g is not None and i == first_round[g]:
+                if g >= RING and g % HALF == 0:
+                    mix_windows(g // HALF)
+                if g == GROUPS - 1:
+                    share_lanes()

@@ -32,6 +32,8 @@ NORM = 1.0 / (D**0.5)
 MASKED = -1.0e10
 MINUS_ONE = -1.0
 E_BUFFERS = 6
+ALL_HEADS = tuple(range(H))
+HEAD_HALVES = (ALL_HEADS[:BATCH], ALL_HEADS[BATCH:])
 
 ORDER = list(range(2, GROUPS)) + [1, 0]
 FIRST_GROUP = ORDER[0]
@@ -123,9 +125,11 @@ def tile_sparseselfattention_pa_kernel(tc, q_rot, k_rot, v, out):
         k_rows = {}
         v_rows = {}
 
-        def load_rows(rows, src, name, g):
-            rows[g] = const.tile([P, H * D], BF16, name="%s_rows_%d" % (name, g))
-            nc.sync.dma_start(out=rows[g][:], in_=src[g * P : (g + 1) * P, :])
+        def load_rows(rows, src, name, g, heads=ALL_HEADS):
+            cols = slice(heads[0] * D, (heads[-1] + 1) * D)
+            if g not in rows:
+                rows[g] = const.tile([P, H * D], BF16, name="%s_rows_%d" % (name, g))
+            nc.sync.dma_start(out=rows[g][:, cols], in_=src[g * P : (g + 1) * P, cols])
 
         def load_window(w):
             v_rows[w] = work.tile([P, PACK, H * D], BF16, name="v_rows", bufs=WINDOWS - 1)
@@ -134,8 +138,13 @@ def tile_sparseselfattention_pa_kernel(tc, q_rot, k_rot, v, out):
                 in_=v2d[w * K_PASS : (w + 1) * K_PASS, :].rearrange("(p j) c -> p j c", j=PACK),
             )
 
+        for heads in HEAD_HALVES:
+            load_rows(q_rows, q2d, "q", FIRST_GROUP, heads)
+            for b in range(FIRST_GROUP + 1):
+                load_rows(k_rows, k2d, "k", b, heads)
         for g in ORDER:
-            load_rows(q_rows, q2d, "q", g)
+            if g not in q_rows:
+                load_rows(q_rows, q2d, "q", g)
             for b in range(g + 1):
                 if b not in k_rows:
                     load_rows(k_rows, k2d, "k", b)
@@ -171,7 +180,10 @@ def tile_sparseselfattention_pa_kernel(tc, q_rot, k_rot, v, out):
         for n in range(E_BUFFERS):
             for one in (False, True):
                 e_tiles[one, n] = const.tile([P, LANES * K_PASS], BF16, name="e_%d_%d" % (one, n))
-            nc.vector.memset(e_tiles[False, n][:], 0.0)
+            words = e_tiles[False, n][:].bitcast(F32).rearrange(
+                "q (u l p) -> q u l p", u=PLANES, l=LANES
+            )
+            nc.vector.memset(words[:, :, :, P - QUADRANT :], 0.0)
             words = e_tiles[True, n][:].bitcast(F32).rearrange("q (u x) -> q u x", u=PLANES)
             nc.gpsimd.memset(words[:, :, P + QUADRANT :], 0.0)
 
@@ -211,22 +223,31 @@ def tile_sparseselfattention_pa_kernel(tc, q_rot, k_rot, v, out):
         def e_tile(j):
             return e_tiles[one_head(j), j % E_BUFFERS]
 
-        def turn(rows, out_tile):
+        def turn(rows, heads):
             bank = turn_banks.tile([P, H, P], BF16, tag="turn", name="rows_bank")
-            for h in range(H):
+            for h in heads:
                 nc.tensor.transpose(bank[:, h, :], rows[:, h * D : (h + 1) * D], ident_bf[:])
-            nc.scalar.copy(out=out_tile[:], in_=bank[:])
+            return bank
 
-        def turn_q(g):
-            q_turned[g] = turned.tile([P, H, P], BF16, name="qT", bufs=3)
-            turn(q_rows[g], q_turned[g])
+        def copy_q(g, bank, heads=ALL_HEADS, copy=nc.scalar.copy):
+            part = slice(heads[0], heads[-1] + 1)
+            if g not in q_turned:
+                q_turned[g] = turned.tile([P, H, P], BF16, name="qT", bufs=3)
+            copy(out=q_turned[g][:, part, :], in_=bank[:, part, :])
 
-        def turn_k(b):
-            if b < FIRST_GROUP:
-                k_turned[b] = const.tile([P, H, P], BF16, name="kT_%d" % b)
-            else:
-                k_turned[b] = turned.tile([P, H, P], BF16, name="kT", bufs=RING + 1)
-            turn(k_rows[b], k_turned[b])
+        def copy_k(b, bank, heads=ALL_HEADS, copy=nc.scalar.copy):
+            if b not in k_turned:
+                if b < FIRST_GROUP:
+                    k_turned[b] = const.tile([P, H, P], BF16, name="kT_%d" % b)
+                else:
+                    k_turned[b] = turned.tile([P, H, P], BF16, name="kT", bufs=RING + 1)
+            part = slice(heads[0], heads[-1] + 1)
+            copy(out=k_turned[b][:, part, :], in_=bank[:, part, :])
+
+        def turn_first(heads):
+            copy_q(FIRST_GROUP, turn(q_rows[FIRST_GROUP], heads), heads, nc.vector.tensor_copy)
+            for b in range(FIRST_GROUP + 1):
+                copy_k(b, turn(k_rows[b], heads), heads, nc.vector.tensor_copy if b % 2 else nc.scalar.copy)
 
         def scores(j, lane):
             g, lanes = units[j]
@@ -405,23 +426,20 @@ def tile_sparseselfattention_pa_kernel(tc, q_rot, k_rot, v, out):
                 in_=result[:].rearrange("q h d -> q (h d)"),
             )
 
-        turns = {}
+        q_turns = {}
+        k_turns = {}
         for g, following in zip(ORDER, ORDER[1:]):
             start = first_round[g]
             if following > g:
-                turns[start, 0] = (turn_q, following)
-                turns[(start + 1, 0) if g >= HALF else (start, 1)] = (turn_k, following)
+                q_turns[start] = following
+                k_turns[(start + 1, 0) if g >= HALF else (start, 1)] = following
         for n, g in enumerate(ORDER[ORDER.index(GROUPS - 1) + 1 :]):
-            turns[first_round[GROUPS - 1] + n, 0] = (turn_q, g)
+            q_turns[first_round[GROUPS - 1] + n] = g
 
-        def turn_rows(i, place):
-            if (i, place) in turns:
-                call, g = turns[i, place]
-                call(g)
+        def copied_by_vector(g):
+            return g % 2 == 0
 
-        turn_q(FIRST_GROUP)
-        for b in range(FIRST_GROUP + 1):
-            turn_k(b)
+        turn_first(HEAD_HALVES[0])
         for i in range(len(rounds) + LAG_PV):
             a, b = unit(i, 0), unit(i, 1)
             g = units[a][0] if a is not None else None
@@ -436,7 +454,14 @@ def tile_sparseselfattention_pa_kernel(tc, q_rot, k_rot, v, out):
             if a is not None:
                 scores(a, 1)
                 negate_and_minimum(a, 1)
-            turn_rows(i, 0)
+            if i == 0:
+                turn_first(HEAD_HALVES[1])
+            if i in q_turns:
+                q_bank = turn(q_rows[q_turns[i]], ALL_HEADS)
+                if not copied_by_vector(q_turns[i]):
+                    copy_q(q_turns[i], q_bank)
+            if (i, 0) in k_turns:
+                copy_k(k_turns[i, 0], turn(k_rows[k_turns[i, 0]], ALL_HEADS))
             if b is not None:
                 scores(b, 0)
                 negate_and_minimum(b, 0)
@@ -445,6 +470,8 @@ def tile_sparseselfattention_pa_kernel(tc, q_rot, k_rot, v, out):
                 regroup_e(i - LAG_TURN, 1)
             if unit(i - LAG_QUANT, 0) is not None:
                 quantise_e(i - LAG_QUANT)
+            if i in q_turns and copied_by_vector(q_turns[i]):
+                copy_q(q_turns[i], q_bank, copy=nc.vector.tensor_copy)
             if i - 1 in v_steps:
                 quantise_v(*v_steps[i - 1])
             if i in v_steps:
@@ -466,7 +493,8 @@ def tile_sparseselfattention_pa_kernel(tc, q_rot, k_rot, v, out):
             for done in ORDER:
                 if last_round[done] == i - 1:
                     invert_sums(done)
-            turn_rows(i, 1)
+            if (i, 1) in k_turns:
+                copy_k(k_turns[i, 1], turn(k_rows[k_turns[i, 1]], ALL_HEADS))
             if g is not None and i == first_round[g]:
                 if g >= RING and g % HALF == 0:
                     mix_windows(g // HALF)

from contextlib import ExitStack

import concourse.mybir as mybir
from concourse.masks import make_identity

BF16 = mybir.dt.bfloat16
F32 = mybir.dt.float32
I32 = mybir.dt.int32
U32 = mybir.dt.uint32
U8 = mybir.dt.uint8
FP8X4 = mybir.dt.float8_e4m3fn_x4
ALU = mybir.AluOpType
ACT = mybir.ActivationFunctionType

S = 2048
H = 8
D = 128
P = 128
PACK = 4
WORD = 4
GROUPS = S // P
RING = 8
HALF = 4
K_PASS = HALF * P
QUADRANT = 32
LANES = 2
PLANES = 2
PAIR = 2
BATCH = 4
WINDOWS = S // K_PASS
NORM = 1.0 / (D**0.5)
MASKED = -1.0e10
MINUS_ONE = -1.0
E_BUFFERS = 6
ALL_HEADS = tuple(range(H))
HEAD_HALVES = (ALL_HEADS[:BATCH], ALL_HEADS[BATCH:])

ORDER = list(range(2, GROUPS)) + [1, 0]
FIRST_GROUP = ORDER[0]

LAG_TURN = 2
LAG_QUANT = 3
LAG_PV = 4

FLOPS = 2 * 2 * H * P * D * (4 * K_PASS + 12 * 2 * K_PASS)


def ring_block(g, slot):
    return g - (g - slot) % RING


def heads_of_lane(g):
    return HALF // (g + 1) if g < HALF else 1


def units_of(g):
    if g >= HALF:
        return [(g, (((h,), 0), ((h,), 1))) for h in range(H)]
    n = heads_of_lane(g)
    lanes = [(tuple(range(h, h + n)), 0) for h in range(0, H, n)]
    return [(g, (lanes[i], lanes[i + 1])) for i in range(0, len(lanes), LANES)]


def lane_blocks(g, lane):
    heads, half = lane
    if g < HALF:
        return [(h, b, i * (g + 1) + b) for i, h in enumerate(heads) for b in range(g + 1)]
    ring = [(ring_block(g, half * HALF + s), s) for s in range(HALF)]
    return [(heads[0], b, s) for b, s in ring if b >= 0]


def lane_pieces(g, lane):
    slots = {}
    for h, b, s in lane_blocks(g, lane):
        slots.setdefault(h, []).append(s)
    return [(h, min(ss) * P, len(ss) * P) for h, ss in slots.items()]


def tile_sparseselfattention_pa_kernel(tc, q_rot, k_rot, v, out):
    nc = tc.nc
    q2d = q_rot.rearrange("s b h d -> s (b h d)")
    k2d = k_rot.rearrange("s b h d -> s (b h d)")
    v2d = v.rearrange("s b h d -> s (b h d)")
    out2d = out.rearrange("s b c -> s (b c)")

    units = []
    rounds = []
    first_round = {}
    last_round = {}
    for g in ORDER:
        of_group = units_of(g)
        first_round[g] = len(rounds)
        for n in range(0, len(of_group), 2):
            pair = of_group[n : n + 2]
            rounds.append(list(range(len(units), len(units) + len(pair))))
            units.extend(pair)
        last_round[g] = len(rounds) - 1

    def unit(i, k):
        return rounds[i][k] if 0 <= i < len(rounds) and k < len(rounds[i]) else None

    def one_head(j):
        return units[j][0] >= HALF

    def heads_of(j):
        return sorted(set(h for heads, half in units[j][1] for h in heads))

    v_steps = {}
    for w in range(WINDOWS):
        start = w * H // 2 if w < LANES else first_round[w * HALF - 2]
        for n in range(H // 2):
            v_steps[start + n] = (w, (2 * n, 2 * n + 1))

    with ExitStack() as ctx:
        const = ctx.enter_context(tc.tile_pool(name="const", bufs=1))
        turned = ctx.enter_context(tc.tile_pool(name="turned", bufs=2))
        work = ctx.enter_context(tc.tile_pool(name="work", bufs=2))
        small = ctx.enter_context(tc.tile_pool(name="small", bufs=6))
        score_banks = ctx.enter_context(tc.psum_pool(name="score_banks", bufs=3))
        turn_banks = ctx.enter_context(tc.psum_pool(name="turn_banks", bufs=3))
        ctx_banks = ctx.enter_context(tc.psum_pool(name="ctx_banks", bufs=2))
        ctx.enter_context(tc.manual_schedule())

        q_rows = {}
        k_rows = {}
        v_rows = {}

        def load_rows(rows, src, name, g, heads=ALL_HEADS):
            cols = slice(heads[0] * D, (heads[-1] + 1) * D)
            if g not in rows:
                rows[g] = const.tile([P, H * D], BF16, name="%s_rows_%d" % (name, g))
            nc.sync.dma_start(out=rows[g][:, cols], in_=src[g * P : (g + 1) * P, cols])

        def load_window(w):
            v_rows[w] = work.tile([P, PACK, H * D], BF16, name="v_rows", bufs=WINDOWS - 1)
            nc.sync.dma_start(
                out=v_rows[w][:],
                in_=v2d[w * K_PASS : (w + 1) * K_PASS, :].rearrange("(p j) c -> p j c", j=PACK),
            )

        for heads in HEAD_HALVES:
            load_rows(q_rows, q2d, "q", FIRST_GROUP, heads)
            for b in range(FIRST_GROUP + 1):
                load_rows(k_rows, k2d, "k", b, heads)
        for g in ORDER:
            if g not in q_rows:
                load_rows(q_rows, q2d, "q", g)
            for b in range(g + 1):
                if b not in k_rows:
                    load_rows(k_rows, k2d, "k", b)
            if FIRST_GROUP < g < FIRST_GROUP + WINDOWS:
                load_window(g - FIRST_GROUP - 1)
        load_window(WINDOWS - 1)

        warm = const.tile([P, 1], F32)
        nc.vector.memset(warm[:], 0.0)
        nc.scalar.activation(out=warm[:], in_=warm[:], func=ACT.Exp)

        ident_bf = const.tile([P, P], BF16)
        make_identity(nc, ident_bf[:])
        ident_f32 = const.tile([P, P], F32)
        make_identity(nc, ident_f32[:])
        causal_f32 = const.tile([P, P], F32)
        nc.gpsimd.memset(causal_f32[:], 0.0)
        nc.gpsimd.affine_select(
            out=causal_f32[:],
            in_=causal_f32[:],
            compare_op=ALU.is_ge,
            fill=MASKED,
            base=0,
            pattern=[[-1, P]],
            channel_multiplier=1,
        )
        causal_bf = const.tile([P, P], BF16)
        nc.vector.tensor_copy(out=causal_bf[:], in_=causal_f32[:])
        minus_one = const.tile([P, H], F32)
        nc.gpsimd.memset(minus_one[:], MINUS_ONE)

        e_tiles = {}
        for n in range(E_BUFFERS):
            for one in (False, True):
                e_tiles[one, n] = const.tile([P, LANES * K_PASS], BF16, name="e_%d_%d" % (one, n))
            words = e_tiles[False, n][:].bitcast(F32).rearrange(
                "q (u l p) -> q u l p", u=PLANES, l=LANES
            )
            nc.vector.memset(words[:, :, :, P - QUADRANT :], 0.0)
            words = e_tiles[True, n][:].bitcast(F32).rearrange("q (u x) -> q u x", u=PLANES)
            nc.gpsimd.memset(words[:, :, P + QUADRANT :], 0.0)

        def v_tiles(name):
            return (
                const.tile([P, H * D], U32, align_bytes=64, name="codes_" + name),
                const.tile([P, H * D], U8, align_bytes=64, name="scales_" + name),
            )

        v_windows = [v_tiles("window_%d" % w) for w in range(WINDOWS)]
        v_mixed = {}
        v_shared = {}
        for g in range(HALF):
            if heads_of_lane(g) > 1:
                v_shared[g] = v_tiles("shared_%d" % g)
                for tile in v_shared[g]:
                    nc.gpsimd.memset(tile[:].bitcast(I32), 0)

        q_turned = {}
        k_turned = {}
        banks = {}
        negated = {}
        minima = {}
        lowest = {}
        row_sums = {}
        inverse = {}
        e_turned = {}
        e_grouped = {}
        e_codes = {}
        e_scales = {}
        ctx_bank = {}
        v_grouped = {}

        def by_plane(tile):
            return tile[:].rearrange("q (u l p e) -> q u l p e", u=PLANES, l=LANES, e=PAIR)

        def e_tile(j):
            return e_tiles[one_head(j), j % E_BUFFERS]

        def turn(rows, heads):
            bank = turn_banks.tile([P, H, P], BF16, tag="turn", name="rows_bank")
            for h in heads:
                nc.tensor.transpose(bank[:, h, :], rows[:, h * D : (h + 1) * D], ident_bf[:])
            return bank

        def copy_q(g, bank, heads=ALL_HEADS, copy=nc.scalar.copy):
            part = slice(heads[0], heads[-1] + 1)
            if g not in q_turned:
                q_turned[g] = turned.tile([P, H, P], BF16, name="qT", bufs=3)
            copy(out=q_turned[g][:, part, :], in_=bank[:, part, :])

        def copy_k(b, bank, heads=ALL_HEADS, copy=nc.scalar.copy):
            if b not in k_turned:
                if b < FIRST_GROUP:
                    k_turned[b] = const.tile([P, H, P], BF16, name="kT_%d" % b)
                else:
                    k_turned[b] = turned.tile([P, H, P], BF16, name="kT", bufs=RING + 1)
            part = slice(heads[0], heads[-1] + 1)
            copy(out=k_turned[b][:, part, :], in_=bank[:, part, :])

        def turn_first(heads):
            copy_q(FIRST_GROUP, turn(q_rows[FIRST_GROUP], heads), heads, nc.vector.tensor_copy)
            for b in range(FIRST_GROUP + 1):
                copy_k(b, turn(k_rows[b], heads), heads, nc.vector.tensor_copy if b % 2 else nc.scalar.copy)

        def scores(j, lane):
            g, lanes = units[j]
            bank = score_banks.tile([P, K_PASS], F32, name="score_bank")
            for h, b, s in lane_blocks(g, lanes[lane]):
                cols = slice(s * P, (s + 1) * P)
                nc.tensor.matmul(
                    bank[:, cols], lhsT=q_turned[g][:, h, :], rhs=k_turned[b][:, h, :],
                    start=True, stop=(b != g),
                )
                if b == g:
                    nc.tensor.matmul(
                        bank[:, cols], lhsT=ident_bf[:], rhs=causal_bf[:], start=False, stop=True
                    )
            banks[j, lane] = bank

        def negate_and_minimum(j, lane):
            g, lanes = units[j]
            if lane == 0:
                negated[j] = work.tile([P, LANES * K_PASS], F32, name="negated", bufs=5)
                minima[j] = small.tile([P, LANES * HALF], F32, name="minima")
            for n, (h, first, width) in enumerate(lane_pieces(g, lanes[lane])):
                column = lane * heads_of_lane(g) + n
                nc.vector.tensor_scalar(
                    out=by_plane(negated[j])[:, :, lane, first // PACK : (first + width) // PACK, :],
                    in0=banks[j, lane][:, first : first + width].rearrange(
                        "q (p u e) -> q u p e", u=PLANES, e=PAIR
                    ),
                    scalar1=-NORM, scalar2=None, op0=ALU.mult, op1=ALU.min,
                    accum_out=minima[j][:, column : column + 1],
                )
            if one_head(j) and lane == LANES - 1:
                lowest[j] = small.tile([P, 1], F32, name="lowest")
                nc.gpsimd.tensor_scalar(
                    out=lowest[j][:], in0=minima[j][:, 0:1], scalar1=minima[j][:, 1:2], scalar2=0.0,
                    op0=ALU.min, op1=ALU.add,
                )

        def exponentials(j):
            g, lanes = units[j]
            if g not in row_sums:
                row_sums[g] = small.tile([P, H], F32, name="row_sums")
            if one_head(j):
                h, first, width = lane_pieces(g, lanes[1])[0]
                run = (K_PASS + width) // PLANES
                nc.scalar.activation(
                    out=e_tile(j)[:].rearrange("q (u x) -> q u x", u=PLANES)[:, :, :run],
                    in_=negated[j][:].rearrange("q (u x) -> q u x", u=PLANES)[:, :, :run],
                    func=ACT.Exp, bias=lowest[j][:], scale=-1.0, accum_out=row_sums[g][:, h : h + 1],
                )
                return
            for lane in range(LANES):
                for n, (h, first, width) in enumerate(lane_pieces(g, lanes[lane])):
                    column = lane * heads_of_lane(g) + n
                    run = slice(first // PLANES, (first + width) // PLANES)
                    nc.scalar.activation(
                        out=e_tile(j)[:].rearrange("q (u l x) -> q u l x", u=PLANES, l=LANES)[:, :, lane, run],
                        in_=negated[j][:].rearrange("q (u l x) -> q u l x", u=PLANES, l=LANES)[:, :, lane, run],
                        func=ACT.Exp, bias=minima[j][:, column : column + 1], scale=-1.0,
                        accum_out=row_sums[g][:, h : h + 1],
                    )

        def turn_e(j):
            e_turned[j] = turn_banks.tile([P, LANES, PLANES, P], F32, tag="turn", name="e_turned")
            words = e_tile(j)[:].bitcast(F32).rearrange("q (u l p) -> q u l p", u=PLANES, l=LANES)
            for lane in range(LANES):
                for u in range(PLANES):
                    nc.tensor.transpose(e_turned[j][:, lane, u, :], words[:, u, lane, :], ident_f32[:])

        def regroup_e(i, k):
            width = LANES * P * PACK
            if k == 0:
                e_grouped[i] = work.tile([P, 2 * width], BF16, align_bytes=64, name="e_grouped")
            nc.scalar.copy(
                out=e_grouped[i][:, k * width : (k + 1) * width]
                .bitcast(F32)
                .rearrange("p (l q u) -> p l q u", l=LANES, u=PLANES),
                in_=e_turned[unit(i, k)][:].rearrange("p l u q -> p l q u"),
            )

        def quantise_e(i):
            words = len(rounds[i]) * LANES * P
            e_codes[i] = work.tile([P, 2 * LANES * P], U32, align_bytes=64, name="e_codes")
            e_scales[i] = work.tile([P, 2 * LANES * P], U8, align_bytes=64, name="e_scales")
            nc.vector.quantize_mx(
                out=e_codes[i][:, :words].bitcast(FP8X4),
                scales=e_scales[i][:, :words],
                in_=e_grouped[i][:, : words * PACK],
            )

        def v_operand(g, half):
            if g in v_shared:
                return v_shared[g]
            blocks = [ring_block(g, half * HALF + s) for s in range(HALF)]
            w = max(blocks) // HALF
            fresh = len([b for b in blocks if b // HALF == w])
            return v_windows[w] if w < LANES or fresh == HALF else v_mixed[w, fresh]

        def e_times_v(i, k):
            j = unit(i, k)
            g, lanes = units[j]
            for lane, (heads, half) in enumerate(lanes):
                batch = (g, heads[0] // BATCH)
                if batch not in ctx_bank:
                    ctx_bank[batch] = ctx_banks.tile([P, BATCH * D], F32, name="ctx_bank")
                codes, scales = v_operand(g, half)
                e_cols = slice((k * LANES + lane) * P, (k * LANES + lane + 1) * P)
                v_cols = slice(heads[0] * D, (heads[-1] + 1) * D)
                first = heads[0] % BATCH
                nc.tensor.matmul_mx(
                    out=ctx_bank[batch][:, first * D : (first + len(heads)) * D],
                    lhsT=e_codes[i][:, e_cols].bitcast(FP8X4),
                    lhsT_scale=e_scales[i][:, e_cols],
                    rhs=codes[:, v_cols].bitcast(FP8X4),
                    rhs_scale=scales[:, v_cols],
                    start=(lane == 0 or not one_head(j)),
                    stop=(lane == LANES - 1 or not one_head(j)),
                )

        def regroup_v(w, heads):
            cols = slice(heads[0] * D, (heads[-1] + 1) * D)
            v_grouped[w, heads] = work.tile(
                [P, len(heads) * D, PACK], BF16, align_bytes=64, name="v_grouped", bufs=1
            )
            nc.gpsimd.tensor_scalar(
                out=v_grouped[w, heads][:], in0=v_rows[w][:, :, cols].rearrange("p j c -> p c j"),
                scalar1=1.0, scalar2=0.0, op0=ALU.mult, op1=ALU.add,
            )

        def quantise_v(w, heads):
            cols = slice(heads[0] * D, (heads[-1] + 1) * D)
            codes, scales = v_windows[w]
            nc.vector.quantize_mx(
                out=codes[:, cols].bitcast(FP8X4),
                scales=scales[:, cols],
                in_=v_grouped[w, heads][:].rearrange("p c j -> p (c j)"),
            )

        def mix_windows(w):
            for fresh in range(1, HALF):
                v_mixed[w, fresh] = v_tiles("mixed_%d" % fresh)
                for src, rows in ((w, slice(0, QUADRANT * fresh)), (w - LANES, slice(QUADRANT * fresh, P))):
                    for to, of in zip(v_mixed[w, fresh], v_windows[src]):
                        nc.sync.dma_start(out=to[rows, :].bitcast(I32), in_=of[rows, :].bitcast(I32))

        def share_lanes():
            for g, shared in v_shared.items():
                n_heads = heads_of_lane(g)
                rows = QUADRANT * (g + 1)
                for n in range(n_heads):
                    for to, of in zip(shared, v_windows[0]):
                        nc.sync.dma_start(
                            out=to[n * rows : (n + 1) * rows, :]
                            .bitcast(I32)
                            .rearrange("p (l n x) -> p l n x", l=H // n_heads, n=n_heads)[:, :, n, :],
                            in_=of[0:rows, :]
                            .bitcast(I32)
                            .rearrange("p (l n x) -> p l n x", l=H // n_heads, n=n_heads)[:, :, n, :],
                        )

        def invert_sums(g):
            inverse[g] = small.tile([P, H], F32, name="inverse")
            nc.gpsimd.tensor_tensor(out=inverse[g][:], in0=row_sums[g][:], in1=minus_one[:], op=ALU.pow)

        def divide_and_store(g, part):
            heads = slice(part * BATCH, (part + 1) * BATCH)
            result = work.tile([P, BATCH, D], F32, name="result", bufs=3)
            nc.vector.tensor_tensor(
                out=result[:],
                in0=ctx_bank[g, part][:].rearrange("q (h d) -> q h d", h=BATCH),
                in1=inverse[g][:, heads].unsqueeze(2).to_broadcast([P, BATCH, D]),
                op=ALU.mult,
            )
            nc.sync.dma_start(
                out=out2d[g * P : (g + 1) * P, part * BATCH * D : (part + 1) * BATCH * D],
                in_=result[:].rearrange("q h d -> q (h d)"),
            )

        q_turns = {}
        k_turns = {}
        for g, following in zip(ORDER, ORDER[1:]):
            start = first_round[g]
            if following > g:
                q_turns[start] = following
                k_turns[(start + 1, 0) if g >= HALF else (start, 1)] = following
        for n, g in enumerate(ORDER[ORDER.index(GROUPS - 1) + 1 :]):
            q_turns[first_round[GROUPS - 1] + n] = g

        def copied_by_vector(g):
            return g % 2 == 0

        turn_first(HEAD_HALVES[0])
        for i in range(len(rounds) + LAG_PV):
            a, b = unit(i, 0), unit(i, 1)
            g = units[a][0] if a is not None else None
            if a is not None:
                scores(a, 0)
                negate_and_minimum(a, 0)
            if unit(i - LAG_TURN, 0) is not None:
                turn_e(unit(i - LAG_TURN, 0))
                regroup_e(i - LAG_TURN, 0)
            if unit(i - 1, 1) is not None:
                exponentials(unit(i - 1, 1))
            if a is not None:
                scores(a, 1)
                negate_and_minimum(a, 1)
            if i == 0:
                turn_first(HEAD_HALVES[1])
            if i in q_turns:
                q_bank = turn(q_rows[q_turns[i]], ALL_HEADS)
                if not copied_by_vector(q_turns[i]):
                    copy_q(q_turns[i], q_bank)
            if (i, 0) in k_turns:
                copy_k(k_turns[i, 0], turn(k_rows[k_turns[i, 0]], ALL_HEADS))
            if b is not None:
                scores(b, 0)
                negate_and_minimum(b, 0)
            if unit(i - LAG_TURN, 1) is not None:
                turn_e(unit(i - LAG_TURN, 1))
                regroup_e(i - LAG_TURN, 1)
            if unit(i - LAG_QUANT, 0) is not None:
                quantise_e(i - LAG_QUANT)
            if i in q_turns and copied_by_vector(q_turns[i]):
                copy_q(q_turns[i], q_bank, copy=nc.vector.tensor_copy)
            if i - 1 in v_steps:
                quantise_v(*v_steps[i - 1])
            if i in v_steps:
                regroup_v(*v_steps[i])
            if a is not None:
                exponentials(a)
            for k in range(2):
                if unit(i - LAG_PV, k) is not None:
                    e_times_v(i - LAG_PV, k)
            if b is not None:
                scores(b, 1)
                negate_and_minimum(b, 1)
            for k in range(2):
                j = unit(i - LAG_PV, k)
                if j is not None:
                    for h in heads_of(j):
                        if h % BATCH == BATCH - 1:
                            divide_and_store(units[j][0], h // BATCH)
            for done in ORDER:
                if last_round[done] == i - 1:
                    invert_sums(done)
            if (i, 1) in k_turns:
                copy_k(k_turns[i, 1], turn(k_rows[k_turns[i, 1]], ALL_HEADS))
            if g is not None and i == first_round[g]:
                if g >= RING and g % HALF == 0:
                    mix_windows(g // HALF)
                if g == GROUPS - 1:
                    share_lanes()
